import numpy as np
import ml_dtypes


def mxq(x, axis, fmt="e4m3"):
    dtype, down = {"e4m3": (ml_dtypes.float8_e4m3fn, 7), "e5m2": (ml_dtypes.float8_e5m2, 14)}[fmt]
    v = np.moveaxis(np.asarray(x, np.float32).astype(ml_dtypes.bfloat16).astype(np.float64), axis, -1)
    blocks = v.reshape(v.shape[:-1] + (-1, 32))
    amax = np.abs(blocks).max(-1, keepdims=True)
    byte = np.maximum(np.where(amax > 0, np.frexp(amax)[1] - 1 + 127, 0) - down, 1)
    scale = np.exp2(byte - 127.0)
    codes = (blocks / scale).astype(np.float32).astype(dtype).astype(np.float64)
    return np.moveaxis((codes * scale).reshape(v.shape), -1, axis)


WIDE = False


def mx_kscale(k):
    if not WIDE:
        return np.ones(k)
    levels = np.array([30, -30])
    if k % 512:
        return np.exp2(np.random.permutation(np.resize(levels, k // 32))).repeat(32)
    a = np.empty((k // 512, 16))
    for p in range(k // 512):
        a[p, :8] = np.random.permutation(np.resize(levels, 8))
        for g in range(8):
            far = levels[np.abs(levels - a[p, g]) >= 10]
            a[p, g + 8] = far[np.random.randint(len(far))]
    return np.exp2(a.ravel()).repeat(32)


BF16 = ml_dtypes.bfloat16


def bf(x):
    return np.asarray(x, np.float32).astype(BF16)


def f64(x):
    return np.asarray(x).astype(np.float64)


B, T, D, H, NUM_LAYERS = 4, 2048, 512, 512, 3
EPS = 1e-8


def setup_inputs():
    s = mx_kscale(D)
    return {"inv": bf(np.random.standard_normal((B, T, D)) * 0.5 * s),
            "Wk": bf(np.random.standard_normal((D, D)) * 2.0 / np.sqrt(D) / s[None, :]),
            "bk": bf(2.5 / np.sqrt(D) + 0.7 * np.random.standard_normal(D))}


def reference(inv, Wk, bk):
    flat = f64(inv).reshape(-1, D)
    out = (mxq(flat, 1, "e5m2") @ mxq(f64(Wk), 1, "e5m2").T) + f64(bk)
    sqrtD = np.sqrt(D)
    S = out.sum(-1, keepdims=True)
    norms = np.sqrt((out * out).sum(-1, keepdims=True))
    c = out * S / (np.maximum(np.abs(out) * sqrtD, EPS) * np.maximum(norms, EPS))
    diff = np.abs(c[1:] - c[:-1]).sum(0)
    return np.broadcast_to(diff, (D, D)).copy()

@@ -1,0 +1,324 @@
+from contextlib import ExitStack
+
+import concourse.mybir as mybir
+from concourse.masks import make_identity
+
+F32 = mybir.dt.float32
+BF16 = mybir.dt.bfloat16
+U32 = mybir.dt.uint32
+U8 = mybir.dt.uint8
+E5X4 = mybir.dt.float8_e5m2_x4
+ALU = mybir.AluOpType
+ACTF = mybir.ActivationFunctionType
+
+P = 128
+D = 512
+TOKENS = 8192
+NT = TOKENS // P
+GT = 4
+NG = NT // GT
+FCH = D // P
+SN = 32
+EPS = 1e-8
+XCAP = EPS / D**0.5
+
+FLOPS = 2 * TOKENS * D * D
+
+
+def tile_dispatcher_pa_kernel(tc, inv, Wk, bk, out):
+    nc = tc.nc
+    flat = inv.flatten_outer_dims().rearrange("(p j) k -> p j k", j=NT)
+
+    with ExitStack() as ctx:
+        const = ctx.enter_context(tc.tile_pool(name="const", bufs=1))
+        rawp = ctx.enter_context(tc.tile_pool(name="rawp", bufs=NG))
+        grpp = ctx.enter_context(tc.tile_pool(name="grpp", bufs=3))
+        codp = ctx.enter_context(tc.tile_pool(name="codp", bufs=3))
+        op = ctx.enter_context(tc.tile_pool(name="op", bufs=2))
+        xp = ctx.enter_context(tc.tile_pool(name="xp", bufs=4))
+        cp = ctx.enter_context(tc.tile_pool(name="cp", bufs=4))
+        ep = ctx.enter_context(tc.tile_pool(name="ep", bufs=10))
+        jp = ctx.enter_context(tc.tile_pool(name="jp", bufs=2))
+        tpp = ctx.enter_context(tc.psum_pool(name="tpp", bufs=3))
+        psp = ctx.enter_context(tc.psum_pool(name="psp", bufs=4))
+        accp = ctx.enter_context(tc.psum_pool(name="accp", bufs=1))
+        ctx.enter_context(tc.manual_schedule())
+
+        wraw = const.tile([P, GT, D], BF16, name="wraw", tag="wraw")
+        nc.sync.dma_start(out=wraw[:], in_=Wk.rearrange("(r p) k -> p r k", p=P))
+        raw = {}
+        for g in range(NG):
+            rt = rawp.tile([P, GT, D], BF16, name="raw", tag="raw")
+            eng = nc.scalar if g == 0 else nc.sync
+            eng.dma_start(out=rt[:], in_=flat[:, g * GT : (g + 1) * GT, :])
+            raw[g] = rt
+
+        ident = const.tile([P, P], F32, name="ident", tag="ident")
+        make_identity(nc, ident[:])
+        bkt = const.tile([P, D], BF16, name="bkt", tag="bkt")
+        nc.gpsimd.dma_start(out=bkt[:], in_=bk.partition_broadcast(P))
+        one = const.tile([P, 1], F32, name="one", tag="one")
+        nc.vector.memset(one[:], 1.0)
+        warm = const.tile([P, 1], F32, name="warm", tag="warm")
+        nc.scalar.activation(out=warm[:], in_=one[:], func=ACTF.Sqrt)
+        zeros = const.tile([P, FCH * SN], F32, name="zeros", tag="zeros")
+        nc.vector.memset(zeros[:], 0.0)
+
+        wsel = const.tile([P, SN], F32, name="wsel", tag="wsel")
+        nc.gpsimd.memset(wsel[:], 0.0)
+        for q in range(P // SN):
+            nc.gpsimd.affine_select(
+                out=wsel[:], in_=wsel[:], compare_op=ALU.not_equal, fill=1.0,
+                base=-SN * q, pattern=[[-1, SN]], channel_multiplier=1,
+            )
+        wcut = const.tile([P, SN], F32, name="wcut", tag="wcut")
+        nc.gpsimd.affine_select(
+            out=wcut[:], in_=wsel[:], compare_op=ALU.not_equal, fill=0.0,
+            base=-(P - 1), pattern=[[0, SN]], channel_multiplier=1,
+        )
+        wtop = const.tile([P, SN], F32, name="wtop", tag="wtop")
+        nc.gpsimd.affine_select(
+            out=wtop[:], in_=wsel[:], compare_op=ALU.is_equal, fill=0.0,
+            base=0, pattern=[[0, SN]], channel_multiplier=1,
+        )
+        shiftm = const.tile([P, P], F32, name="shiftm", tag="shiftm")
+        nc.gpsimd.memset(shiftm[:], 0.0)
+        nc.gpsimd.affine_select(
+            out=shiftm[:], in_=shiftm[:], compare_op=ALU.not_equal, fill=1.0,
+            base=-1, pattern=[[-1, P]], channel_multiplier=1,
+        )
+        wpos = const.tile([P, SN], F32, name="wpos", tag="wpos")
+        nc.vector.tensor_scalar(out=wpos[:], in0=wsel[:], scalar1=2.0, scalar2=None, op0=ALU.mult)
+        wneg = const.tile([P, SN], F32, name="wneg", tag="wneg")
+        nc.vector.tensor_scalar(out=wneg[:], in0=wsel[:], scalar1=-2.0, scalar2=None, op0=ALU.mult)
+        wwrap = const.tile([P, SN], F32, name="wwrap", tag="wwrap")
+        nc.vector.tensor_scalar(out=wwrap[:], in0=wcut[:], scalar1=-2.0, scalar2=None, op0=ALU.mult)
+        wlast = const.tile([P, SN], F32, name="wlast", tag="wlast")
+        nc.vector.tensor_sub(out=wlast[:], in0=wcut[:], in1=wsel[:])
+        wfirst = const.tile([P, SN], F32, name="wfirst", tag="wfirst")
+        nc.vector.tensor_scalar(out=wfirst[:], in0=wtop[:], scalar1=-1.0, scalar2=None, op0=ALU.mult)
+
+        ssum = const.tile([P, NT], F32, name="ssum", tag="ssum")
+        n2 = const.tile([P, NT], F32, name="n2", tag="n2")
+        n2c = const.tile([P, NT], F32, name="n2c", tag="n2c")
+        nrm = const.tile([P, NT], F32, name="nrm", tag="nrm")
+        rec = const.tile([P, NT], F32, name="rec", tag="rec")
+        rr = const.tile([P, NT], F32, name="rr", tag="rr")
+        c0 = const.tile([P, D], F32, name="c0", tag="c0")
+        clast = const.tile([P, D], F32, name="clast", tag="clast")
+        wcodes = const.tile([P, D], U32, name="wcodes", tag="wcodes", align_bytes=64)
+        wscl = const.tile([P, D], U8, name="wscl", tag="wscl", align_bytes=64)
+        acc = accp.tile([P, FCH, SN], F32, name="acc", tag="acc")
+
+        grouped = {}
+        codes = {}
+        scl = {}
+        tps = {}
+        ps = {}
+        o = {}
+        x = {}
+        c = {}
+        e = {}
+
+        def transposes(key, src, t):
+            half = t // 2
+            if t % 2 == 0:
+                tp = tpp.tile([P, 2, 2, P], F32, name="tp", tag="tp")
+                tps[(key, half)] = tp
+            tp = tps[(key, half)]
+            words = src[:].bitcast(F32)
+            for u in range(2):
+                nc.tensor.transpose(tp[:, t % 2, u, :], words[:, t, u : D // 2 : 2], ident[:])
+
+        def evac(key, half):
+            if half == 0:
+                gt = grpp.tile([P, GT * D], BF16, name="grouped", tag="grouped", align_bytes=64)
+                grouped[key] = gt
+            gw = grouped[key][:].bitcast(F32)
+            dst = gw[:, D * half : D * (half + 1)].rearrange("p (t r u) -> p t r u", t=2, u=2)
+            nc.scalar.copy(out=dst, in_=tps[(key, half)][:].rearrange("p t u r -> p t r u"))
+
+        def quant(key, cod, sc):
+            nc.vector.quantize_mx(out=cod[:].bitcast(E5X4), scales=sc[:], in_=grouped[key][:])
+
+        def quant_group(g):
+            cod = codp.tile([P, D], U32, name="codes", tag="codes", align_bytes=64)
+            sc = codp.tile([P, D], U8, name="scl", tag="scl", align_bytes=64)
+            codes[g] = cod
+            scl[g] = sc
+            quant(g, cod, sc)
+
+        def mm(j):
+            g, i = divmod(j, GT)
+            pt = psp.tile([P, D], F32, name="ps", tag="ps")
+            ps[j] = pt
+            cols = slice(i * P, (i + 1) * P)
+            nc.tensor.matmul_mx(
+                out=pt[:],
+                lhsT=codes[g][:, cols].bitcast(E5X4),
+                lhsT_scale=scl[g][:, cols],
+                rhs=wcodes[:].bitcast(E5X4),
+                rhs_scale=wscl[:],
+                start=True,
+                stop=True,
+            )
+
+        def a1(j):
+            g, i = divmod(j, GT)
+            if i == 0:
+                ot = op.tile([P, GT, D], F32, name="o", tag="o")
+                o[g] = ot
+            nc.vector.scalar_tensor_tensor(
+                out=o[g][:, i, :], in0=ps[j][:], scalar=1.0, in1=bkt[:],
+                op0=ALU.mult, op1=ALU.add, accum_out=ssum[:, j : j + 1],
+            )
+
+        def a2(j):
+            g, i = divmod(j, GT)
+            junk = jp.tile([P, D], F32, name="junk", tag="junk")
+            nc.scalar.activation(out=junk[:], in_=o[g][:, i, :], func=ACTF.Square, accum_out=n2[:, j : j + 1])
+
+        def a3(g):
+            xt = xp.tile([P, GT, D], F32, name="x", tag="x")
+            x[g] = xt
+            nc.vector.tensor_scalar(
+                out=xt[:].rearrange("p i d -> p (i d)"), in0=o[g][:].rearrange("p i d -> p (i d)"),
+                scalar1=XCAP, scalar2=-XCAP, op0=ALU.min, op1=ALU.max,
+            )
+
+        def r1(g):
+            cols = slice(g * GT, (g + 1) * GT)
+            nc.scalar.activation(out=n2c[:, cols], in_=n2[:, cols], func=ACTF.Relu, bias=-EPS * EPS)
+            nc.scalar.activation(out=nrm[:, cols], in_=n2c[:, cols], func=ACTF.Sqrt, scale=EPS * EPS, bias=EPS**4)
+
+        def recip(g):
+            cols = slice(g * GT, (g + 1) * GT)
+            nc.vector.reciprocal(out=rec[:, cols], in_=nrm[:, cols])
+
+        def rmul(g):
+            cols = slice(g * GT, (g + 1) * GT)
+            nc.vector.tensor_mul(out=rr[:, cols], in0=rec[:, cols], in1=ssum[:, cols])
+
+        def a4(j, dst):
+            g, i = divmod(j, GT)
+            nc.scalar.activation(out=dst[:], in_=x[g][:, i, :], func=ACTF.Copy, scale=rr[:, j : j + 1])
+
+        def a4_even(j):
+            if j == 0:
+                c[j] = c0
+            else:
+                ct = cp.tile([P, D], F32, name="c", tag="c")
+                c[j] = ct
+            a4(j, c[j])
+
+        def pair(t, other):
+            k = t if t % 2 == 1 else t + 1
+            et = ep.tile([P, D], F32, name="e", tag="e")
+            e[t] = et
+            nc.vector.scalar_tensor_tensor(
+                out=et[:], in0=x[k // GT][:, k % GT, :], scalar=rr[:, k : k + 1], in1=other[:],
+                op0=ALU.mult, op1=(ALU.max if t % 2 == 0 else ALU.min),
+            )
+
+        def sums(src, w):
+            for f in range(FCH):
+                nc.tensor.matmul(
+                    out=acc[:, f, :], lhsT=src[:, f * P : (f + 1) * P], rhs=w[:], start=False, stop=False
+                )
+
+        def sums_e(t):
+            sums(e[t], wpos if t % 2 == 0 else wneg)
+
+        for t in range(GT):
+            transposes("w", wraw, t)
+            if t % 2 == 1:
+                evac("w", t // 2)
+        for t in range(GT):
+            transposes(0, raw[0], t)
+            if t % 2 == 1:
+                evac(0, t // 2)
+        quant("w", wcodes, wscl)
+        quant_group(0)
+        for t in range(2):
+            transposes(1, raw[1], t)
+        evac(1, 0)
+        nc.tensor.matmul(
+            out=acc[:].rearrange("p f n -> p (f n)"), lhsT=ident[:], rhs=zeros[:], start=True, stop=False
+        )
+        for j in range(GT):
+            mm(j)
+        for t in range(2, GT):
+            transposes(1, raw[1], t)
+        evac(1, 1)
+
+        pending = []
+        for s in range(NG + 1):
+            tg = [g for g in ([2, 3] if s == 0 else [s + 3]) if g < NG]
+            if s >= 1:
+                recip(s - 1)
+            if s == NG:
+                c0s = psp.tile([P, D], F32, name="c0s", tag="ps")
+                nc.tensor.matmul(out=c0s[:], lhsT=shiftm[:], rhs=c0[:], start=True, stop=True)
+            for i in range(GT):
+                for g in tg:
+                    transposes(g, raw[g], i)
+                if i < len(pending):
+                    sums_e(pending[i])
+                if s < NG:
+                    a1(s * GT + i)
+                if i == 0 and s >= 1:
+                    rmul(s - 1)
+                if 1 <= s and s + 1 < NG:
+                    mm((s + 1) * GT + i)
+                if s < NG:
+                    a2(s * GT + i)
+                if i == 0 and s >= 1:
+                    a4_even((s - 1) * GT)
+                    a4_even((s - 1) * GT + 2)
+                    if s == NG:
+                        a4(NT - 1, clast)
+                if i == 1:
+                    for g in tg:
+                        evac(g, 0)
+            if s == 2:
+                sums(c0, wfirst)
+            if s < NG:
+                r1(s)
+            for g in tg:
+                evac(g, 1)
+            if s == 0:
+                quant_group(1)
+                for i in range(GT):
+                    mm(GT + i)
+            pending = []
+            if s >= 1:
+                for t in range((s - 1) * GT - 1, (s - 1) * GT + 3):
+                    if t >= 0:
+                        pair(t, c[t + 1 if t % 2 == 1 else t])
+                        pending.append(t)
+            if s < NG:
+                a3(s)
+            if s + 2 < NG:
+                quant_group(s + 2)
+
+        pair(NT - 1, c0s)
+        for t in pending:
+            sums_e(t)
+        sums(clast, wlast)
+        sums(e[NT - 1], wwrap)
+        nc.tensor.matmul(
+            out=acc[:].rearrange("p f n -> p (f n)"), lhsT=ident[:], rhs=zeros[:], start=False, stop=True
+        )
+        tot = const.tile([P, FCH], F32, name="tot", tag="tot")
+        nc.vector.tensor_reduce(out=tot[:], in_=acc[:], axis=mybir.AxisListType.X, op=ALU.add)
+        bc = psp.tile([P, D], F32, name="bc", tag="ps")
+        for f in range(FCH):
+            nc.tensor.matmul(
+                out=bc[:, f * P : (f + 1) * P], lhsT=tot[:, f : f + 1].to_broadcast([P, P]), rhs=ident[:],
+                start=True, stop=True,
+            )
+        res = const.tile([P, D], F32, name="res", tag="res")
+        nc.vector.tensor_copy(out=res[:], in_=bc[:])
+        engs = [nc.sync, nc.scalar, nc.gpsimd, nc.sync]
+        for r in range(D // P):
+            engs[r].dma_start(out=out[r * P : (r + 1) * P, :], in_=res[:])

@@ -18,7 +18,7 @@ NT = TOKENS // P
 GT = 4
 NG = NT // GT
 FCH = D // P
-SN = 32
+MX_REPEAT = 2
 EPS = 1e-8
 XCAP = EPS / D**0.5
 
@@ -39,7 +39,7 @@ def tile_dispatcher_pa_kernel(tc, inv, Wk, bk, out):
         cp = ctx.enter_context(tc.tile_pool(name="cp", bufs=4))
         ep = ctx.enter_context(tc.tile_pool(name="ep", bufs=10))
         jp = ctx.enter_context(tc.tile_pool(name="jp", bufs=2))
-        tpp = ctx.enter_context(tc.psum_pool(name="tpp", bufs=3))
+        tpp = ctx.enter_context(tc.psum_pool(name="tpp", bufs=2))
         psp = ctx.enter_context(tc.psum_pool(name="psp", bufs=4))
         accp = ctx.enter_context(tc.psum_pool(name="accp", bufs=1))
         ctx.enter_context(tc.manual_schedule())
@@ -61,42 +61,29 @@ def tile_dispatcher_pa_kernel(tc, inv, Wk, bk, out):
         nc.vector.memset(one[:], 1.0)
         warm = const.tile([P, 1], F32, name="warm", tag="warm")
         nc.scalar.activation(out=warm[:], in_=one[:], func=ACTF.Sqrt)
-        zeros = const.tile([P, FCH * SN], F32, name="zeros", tag="zeros")
+        zeros = const.tile([P, D], F32, name="zeros", tag="zeros")
         nc.vector.memset(zeros[:], 0.0)
+        ident2 = const.tile([P, P], F32, name="ident2", tag="ident2")
+        nc.vector.tensor_scalar(out=ident2[:], in0=ident[:], scalar1=2.0, scalar2=None, op0=ALU.mult)
 
-        wsel = const.tile([P, SN], F32, name="wsel", tag="wsel")
-        nc.gpsimd.memset(wsel[:], 0.0)
-        for q in range(P // SN):
-            nc.gpsimd.affine_select(
-                out=wsel[:], in_=wsel[:], compare_op=ALU.not_equal, fill=1.0,
-                base=-SN * q, pattern=[[-1, SN]], channel_multiplier=1,
-            )
-        wcut = const.tile([P, SN], F32, name="wcut", tag="wcut")
-        nc.gpsimd.affine_select(
-            out=wcut[:], in_=wsel[:], compare_op=ALU.not_equal, fill=0.0,
-            base=-(P - 1), pattern=[[0, SN]], channel_multiplier=1,
-        )
-        wtop = const.tile([P, SN], F32, name="wtop", tag="wtop")
-        nc.gpsimd.affine_select(
-            out=wtop[:], in_=wsel[:], compare_op=ALU.is_equal, fill=0.0,
-            base=0, pattern=[[0, SN]], channel_multiplier=1,
-        )
         shiftm = const.tile([P, P], F32, name="shiftm", tag="shiftm")
         nc.gpsimd.memset(shiftm[:], 0.0)
         nc.gpsimd.affine_select(
             out=shiftm[:], in_=shiftm[:], compare_op=ALU.not_equal, fill=1.0,
             base=-1, pattern=[[-1, P]], channel_multiplier=1,
         )
-        wpos = const.tile([P, SN], F32, name="wpos", tag="wpos")
-        nc.vector.tensor_scalar(out=wpos[:], in0=wsel[:], scalar1=2.0, scalar2=None, op0=ALU.mult)
-        wneg = const.tile([P, SN], F32, name="wneg", tag="wneg")
-        nc.vector.tensor_scalar(out=wneg[:], in0=wsel[:], scalar1=-2.0, scalar2=None, op0=ALU.mult)
-        wwrap = const.tile([P, SN], F32, name="wwrap", tag="wwrap")
-        nc.vector.tensor_scalar(out=wwrap[:], in0=wcut[:], scalar1=-2.0, scalar2=None, op0=ALU.mult)
-        wlast = const.tile([P, SN], F32, name="wlast", tag="wlast")
-        nc.vector.tensor_sub(out=wlast[:], in0=wcut[:], in1=wsel[:])
-        wfirst = const.tile([P, SN], F32, name="wfirst", tag="wfirst")
-        nc.vector.tensor_scalar(out=wfirst[:], in0=wtop[:], scalar1=-1.0, scalar2=None, op0=ALU.mult)
+        rowfirst = const.tile([P, P], F32, name="rowfirst", tag="rowfirst")
+        nc.gpsimd.memset(rowfirst[:], -1.0)
+        nc.gpsimd.affine_select(
+            out=rowfirst[:], in_=rowfirst[:], compare_op=ALU.is_equal, fill=0.0,
+            base=0, pattern=[[0, P]], channel_multiplier=1,
+        )
+        rowlast = const.tile([P, P], F32, name="rowlast", tag="rowlast")
+        nc.gpsimd.memset(rowlast[:], -1.0)
+        nc.gpsimd.affine_select(
+            out=rowlast[:], in_=rowlast[:], compare_op=ALU.is_equal, fill=0.0,
+            base=-(P - 1), pattern=[[0, P]], channel_multiplier=1,
+        )
 
         ssum = const.tile([P, NT], F32, name="ssum", tag="ssum")
         n2 = const.tile([P, NT], F32, name="n2", tag="n2")
@@ -108,7 +95,8 @@ def tile_dispatcher_pa_kernel(tc, inv, Wk, bk, out):
         clast = const.tile([P, D], F32, name="clast", tag="clast")
         wcodes = const.tile([P, D], U32, name="wcodes", tag="wcodes", align_bytes=64)
         wscl = const.tile([P, D], U8, name="wscl", tag="wscl", align_bytes=64)
-        acc = accp.tile([P, FCH, SN], F32, name="acc", tag="acc")
+        pos = accp.tile([P, FCH, P], F32, name="pos", tag="pos")
+        neg = accp.tile([P, FCH, P], F32, name="neg", tag="neg")
 
         grouped = {}
         codes = {}
@@ -153,15 +141,16 @@ def tile_dispatcher_pa_kernel(tc, inv, Wk, bk, out):
             pt = psp.tile([P, D], F32, name="ps", tag="ps")
             ps[j] = pt
             cols = slice(i * P, (i + 1) * P)
-            nc.tensor.matmul_mx(
-                out=pt[:],
-                lhsT=codes[g][:, cols].bitcast(E5X4),
-                lhsT_scale=scl[g][:, cols],
-                rhs=wcodes[:].bitcast(E5X4),
-                rhs_scale=wscl[:],
-                start=True,
-                stop=True,
-            )
+            for rpt in range(MX_REPEAT):
+                nc.tensor.matmul_mx(
+                    out=pt[:],
+                    lhsT=codes[g][:, cols].bitcast(E5X4),
+                    lhsT_scale=scl[g][:, cols],
+                    rhs=wcodes[:].bitcast(E5X4),
+                    rhs_scale=wscl[:],
+                    start=True,
+                    stop=True,
+                )
 
         def a1(j):
             g, i = divmod(j, GT)
@@ -199,9 +188,9 @@ def tile_dispatcher_pa_kernel(tc, inv, Wk, bk, out):
             cols = slice(g * GT, (g + 1) * GT)
             nc.vector.tensor_mul(out=rr[:, cols], in0=rec[:, cols], in1=ssum[:, cols])
 
-        def a4(j, dst):
+        def a4(j, dst, func):
             g, i = divmod(j, GT)
-            nc.scalar.activation(out=dst[:], in_=x[g][:, i, :], func=ACTF.Copy, scale=rr[:, j : j + 1])
+            nc.scalar.activation(out=dst[:], in_=x[g][:, i, :], func=func, scale=rr[:, j : j + 1])
 
         def a4_even(j):
             if j == 0:
@@ -209,7 +198,7 @@ def tile_dispatcher_pa_kernel(tc, inv, Wk, bk, out):
             else:
                 ct = cp.tile([P, D], F32, name="c", tag="c")
                 c[j] = ct
-            a4(j, c[j])
+            a4(j, c[j], ACTF.Copy)
 
         def pair(t, other):
             k = t if t % 2 == 1 else t + 1
@@ -220,15 +209,18 @@ def tile_dispatcher_pa_kernel(tc, inv, Wk, bk, out):
                 op0=ALU.mult, op1=(ALU.max if t % 2 == 0 else ALU.min),
             )
 
-        def sums(src, w):
+        def acc_e(t):
+            dst = pos if t % 2 == 0 else neg
             for f in range(FCH):
                 nc.tensor.matmul(
-                    out=acc[:, f, :], lhsT=src[:, f * P : (f + 1) * P], rhs=w[:], start=False, stop=False
+                    out=dst[:, f, :], lhsT=e[t][:, f * P : (f + 1) * P], rhs=ident[:], is_transpose=True,
+                    start=False, stop=(t >= NT - 2 and f == FCH - 1),
                 )
 
-        def sums_e(t):
-            sums(e[t], wpos if t % 2 == 0 else wneg)
-
+        for dst in (pos, neg):
+            nc.tensor.matmul(
+                out=dst[:].rearrange("p f n -> p (f n)"), lhsT=ident[:], rhs=zeros[:], start=True, stop=False
+            )
         for t in range(GT):
             transposes("w", wraw, t)
             if t % 2 == 1:
@@ -242,9 +234,6 @@ def tile_dispatcher_pa_kernel(tc, inv, Wk, bk, out):
         for t in range(2):
             transposes(1, raw[1], t)
         evac(1, 0)
-        nc.tensor.matmul(
-            out=acc[:].rearrange("p f n -> p (f n)"), lhsT=ident[:], rhs=zeros[:], start=True, stop=False
-        )
         for j in range(GT):
             mm(j)
         for t in range(2, GT):
@@ -259,33 +248,33 @@ def tile_dispatcher_pa_kernel(tc, inv, Wk, bk, out):
             if s == NG:
                 c0s = psp.tile([P, D], F32, name="c0s", tag="ps")
                 nc.tensor.matmul(out=c0s[:], lhsT=shiftm[:], rhs=c0[:], start=True, stop=True)
-            for i in range(GT):
+            for h in range(2):
+                two = (2 * h, 2 * h + 1)
                 for g in tg:
-                    transposes(g, raw[g], i)
-                if i < len(pending):
-                    sums_e(pending[i])
-                if s < NG:
-                    a1(s * GT + i)
-                if i == 0 and s >= 1:
-                    rmul(s - 1)
-                if 1 <= s and s + 1 < NG:
-                    mm((s + 1) * GT + i)
-                if s < NG:
-                    a2(s * GT + i)
-                if i == 0 and s >= 1:
-                    a4_even((s - 1) * GT)
-                    a4_even((s - 1) * GT + 2)
-                    if s == NG:
-                        a4(NT - 1, clast)
-                if i == 1:
-                    for g in tg:
-                        evac(g, 0)
-            if s == 2:
-                sums(c0, wfirst)
-            if s < NG:
-                r1(s)
-            for g in tg:
-                evac(g, 1)
+                    for i in two:
+                        transposes(g, raw[g], i)
+                for t in pending[2 * h : 2 * h + 2]:
+                    acc_e(t)
+                for i in two:
+                    if s < NG:
+                        a1(s * GT + i)
+                    if i == 0 and s >= 1:
+                        rmul(s - 1)
+                for i in two:
+                    if 1 <= s and s + 1 < NG:
+                        mm((s + 1) * GT + i)
+                for i in two:
+                    if s < NG:
+                        a2(s * GT + i)
+                    if i == 0 and s >= 1:
+                        a4_even((s - 1) * GT)
+                        a4_even((s - 1) * GT + 2)
+                        if s == NG:
+                            a4(NT - 1, clast, ACTF.Abs)
+                if h == 1 and s < NG:
+                    r1(s)
+                for g in tg:
+                    evac(g, h)
             if s == 0:
                 quant_group(1)
                 for i in range(GT):
@@ -303,19 +292,21 @@ def tile_dispatcher_pa_kernel(tc, inv, Wk, bk, out):
 
         pair(NT - 1, c0s)
         for t in pending:
-            sums_e(t)
-        sums(clast, wlast)
-        sums(e[NT - 1], wwrap)
-        nc.tensor.matmul(
-            out=acc[:].rearrange("p f n -> p (f n)"), lhsT=ident[:], rhs=zeros[:], start=False, stop=True
-        )
-        tot = const.tile([P, FCH], F32, name="tot", tag="tot")
-        nc.vector.tensor_reduce(out=tot[:], in_=acc[:], axis=mybir.AxisListType.X, op=ALU.add)
+            acc_e(t)
+        acc_e(NT - 1)
         bc = psp.tile([P, D], F32, name="bc", tag="ps")
+        nc.tensor.matmul(out=bc[:], lhsT=rowfirst[:], rhs=c0[:], start=True, stop=False)
+        nc.tensor.matmul(out=bc[:], lhsT=rowlast[:], rhs=clast[:], start=False, stop=False)
+        redp = const.tile([P, FCH], F32, name="redp", tag="redp")
+        nc.vector.tensor_reduce(out=redp[:], in_=pos[:], axis=mybir.AxisListType.X, op=ALU.add)
+        redn = const.tile([P, FCH], F32, name="redn", tag="redn")
+        nc.vector.tensor_reduce(out=redn[:], in_=neg[:], axis=mybir.AxisListType.X, op=ALU.add)
+        tot = const.tile([P, FCH], F32, name="tot", tag="tot")
+        nc.vector.tensor_sub(out=tot[:], in0=redp[:], in1=redn[:])
         for f in range(FCH):
             nc.tensor.matmul(
-                out=bc[:, f * P : (f + 1) * P], lhsT=tot[:, f : f + 1].to_broadcast([P, P]), rhs=ident[:],
-                start=True, stop=True,
+                out=bc[:, f * P : (f + 1) * P], lhsT=tot[:, f : f + 1].to_broadcast([P, P]), rhs=ident2[:],
+                start=False, stop=(f == FCH - 1),
             )
         res = const.tile([P, D], F32, name="res", tag="res")
         nc.vector.tensor_copy(out=res[:], in_=bc[:])

@@ -19,6 +19,7 @@ GT = 4
 NG = NT // GT
 FCH = D // P
 MX_REPEAT = 2
+G_TILES = 3
 EPS = 1e-8
 XCAP = EPS / D**0.5
 
@@ -45,13 +46,18 @@ def tile_dispatcher_pa_kernel(tc, inv, Wk, bk, out):
         ctx.enter_context(tc.manual_schedule())
 
         wraw = const.tile([P, GT, D], BF16, name="wraw", tag="wraw")
-        nc.sync.dma_start(out=wraw[:], in_=Wk.rearrange("(r p) k -> p r k", p=P))
+        wview = Wk.rearrange("(r p) k -> p r k", p=P)
+        for h in range(2):
+            nc.sync.dma_start(out=wraw[:, 2 * h : 2 * h + 2, :], in_=wview[:, 2 * h : 2 * h + 2, :])
         raw = {}
         for g in range(NG):
             rt = rawp.tile([P, GT, D], BF16, name="raw", tag="raw")
-            eng = nc.scalar if g == 0 else nc.sync
-            eng.dma_start(out=rt[:], in_=flat[:, g * GT : (g + 1) * GT, :])
             raw[g] = rt
+            if g == 0:
+                for h in range(2):
+                    nc.sync.dma_start(out=rt[:, 2 * h : 2 * h + 2, :], in_=flat[:, 2 * h : 2 * h + 2, :])
+            else:
+                nc.sync.dma_start(out=rt[:], in_=flat[:, g * GT : (g + 1) * GT, :])
 
         ident = const.tile([P, P], F32, name="ident", tag="ident")
         make_identity(nc, ident[:])
@@ -63,8 +69,6 @@ def tile_dispatcher_pa_kernel(tc, inv, Wk, bk, out):
         nc.scalar.activation(out=warm[:], in_=one[:], func=ACTF.Sqrt)
         zeros = const.tile([P, D], F32, name="zeros", tag="zeros")
         nc.vector.memset(zeros[:], 0.0)
-        ident2 = const.tile([P, P], F32, name="ident2", tag="ident2")
-        nc.vector.tensor_scalar(out=ident2[:], in0=ident[:], scalar1=2.0, scalar2=None, op0=ALU.mult)
 
         shiftm = const.tile([P, P], F32, name="shiftm", tag="shiftm")
         nc.gpsimd.memset(shiftm[:], 0.0)
@@ -73,13 +77,13 @@ def tile_dispatcher_pa_kernel(tc, inv, Wk, bk, out):
             base=-1, pattern=[[-1, P]], channel_multiplier=1,
         )
         rowfirst = const.tile([P, P], F32, name="rowfirst", tag="rowfirst")
-        nc.gpsimd.memset(rowfirst[:], -1.0)
+        nc.gpsimd.memset(rowfirst[:], -0.5)
         nc.gpsimd.affine_select(
             out=rowfirst[:], in_=rowfirst[:], compare_op=ALU.is_equal, fill=0.0,
             base=0, pattern=[[0, P]], channel_multiplier=1,
         )
         rowlast = const.tile([P, P], F32, name="rowlast", tag="rowlast")
-        nc.gpsimd.memset(rowlast[:], -1.0)
+        nc.gpsimd.memset(rowlast[:], -0.5)
         nc.gpsimd.affine_select(
             out=rowlast[:], in_=rowlast[:], compare_op=ALU.is_equal, fill=0.0,
             base=-(P - 1), pattern=[[0, P]], channel_multiplier=1,
@@ -118,13 +122,17 @@ def tile_dispatcher_pa_kernel(tc, inv, Wk, bk, out):
             for u in range(2):
                 nc.tensor.transpose(tp[:, t % 2, u, :], words[:, t, u : D // 2 : 2], ident[:])
 
-        def evac(key, half):
+        def evac(key, half, on_vector=False):
             if half == 0:
                 gt = grpp.tile([P, GT * D], BF16, name="grouped", tag="grouped", align_bytes=64)
                 grouped[key] = gt
             gw = grouped[key][:].bitcast(F32)
             dst = gw[:, D * half : D * (half + 1)].rearrange("p (t r u) -> p t r u", t=2, u=2)
-            nc.scalar.copy(out=dst, in_=tps[(key, half)][:].rearrange("p t u r -> p t r u"))
+            src = tps[(key, half)][:].rearrange("p t u r -> p t r u")
+            if on_vector:
+                nc.vector.tensor_copy(out=dst, in_=src)
+            else:
+                nc.scalar.copy(out=dst, in_=src)
 
         def quant(key, cod, sc):
             nc.vector.quantize_mx(out=cod[:].bitcast(E5X4), scales=sc[:], in_=grouped[key][:])
@@ -134,14 +142,22 @@ def tile_dispatcher_pa_kernel(tc, inv, Wk, bk, out):
             sc = codp.tile([P, D], U8, name="scl", tag="scl", align_bytes=64)
             codes[g] = cod
             scl[g] = sc
-            quant(g, cod, sc)
+            if g == 0:
+                for h in range(2):
+                    cols = slice(h * D // 2, (h + 1) * D // 2)
+                    nc.vector.quantize_mx(
+                        out=cod[:, cols].bitcast(E5X4), scales=sc[:, cols],
+                        in_=grouped[g][:, h * 2 * D : (h + 1) * 2 * D],
+                    )
+            else:
+                quant(g, cod, sc)
 
         def mm(j):
             g, i = divmod(j, GT)
             pt = psp.tile([P, D], F32, name="ps", tag="ps")
             ps[j] = pt
             cols = slice(i * P, (i + 1) * P)
-            for rpt in range(MX_REPEAT):
+            for rpt in range(1 if j == 0 else MX_REPEAT):
                 nc.tensor.matmul_mx(
                     out=pt[:],
                     lhsT=codes[g][:, cols].bitcast(E5X4),
@@ -167,11 +183,20 @@ def tile_dispatcher_pa_kernel(tc, inv, Wk, bk, out):
             junk = jp.tile([P, D], F32, name="junk", tag="junk")
             nc.scalar.activation(out=junk[:], in_=o[g][:, i, :], func=ACTF.Square, accum_out=n2[:, j : j + 1])
 
+        def a3g(j):
+            g, i = divmod(j, GT)
+            if i == 0:
+                xt = xp.tile([P, GT, D], F32, name="x", tag="x")
+                x[g] = xt
+            if i < G_TILES:
+                nc.gpsimd.tensor_scalar(
+                    out=x[g][:, i, :], in0=o[g][:, i, :], scalar1=XCAP, scalar2=-XCAP, op0=ALU.min, op1=ALU.max
+                )
+
         def a3(g):
-            xt = xp.tile([P, GT, D], F32, name="x", tag="x")
-            x[g] = xt
             nc.vector.tensor_scalar(
-                out=xt[:].rearrange("p i d -> p (i d)"), in0=o[g][:].rearrange("p i d -> p (i d)"),
+                out=x[g][:, G_TILES:, :].rearrange("p i d -> p (i d)"),
+                in0=o[g][:, G_TILES:, :].rearrange("p i d -> p (i d)"),
                 scalar1=XCAP, scalar2=-XCAP, op0=ALU.min, op1=ALU.max,
             )
 
@@ -217,14 +242,16 @@ def tile_dispatcher_pa_kernel(tc, inv, Wk, bk, out):
                     start=False, stop=(t >= NT - 2 and f == FCH - 1),
                 )
 
-        for dst in (pos, neg):
+        def zero_init(dst):
             nc.tensor.matmul(
                 out=dst[:].rearrange("p f n -> p (f n)"), lhsT=ident[:], rhs=zeros[:], start=True, stop=False
             )
+
+        zero_init(pos)
         for t in range(GT):
             transposes("w", wraw, t)
             if t % 2 == 1:
-                evac("w", t // 2)
+                evac("w", t // 2, on_vector=(t == 3))
         for t in range(GT):
             transposes(0, raw[0], t)
             if t % 2 == 1:
@@ -239,6 +266,7 @@ def tile_dispatcher_pa_kernel(tc, inv, Wk, bk, out):
         for t in range(2, GT):
             transposes(1, raw[1], t)
         evac(1, 1)
+        zero_init(neg)
 
         pending = []
         for s in range(NG + 1):
@@ -258,6 +286,7 @@ def tile_dispatcher_pa_kernel(tc, inv, Wk, bk, out):
                 for i in two:
                     if s < NG:
                         a1(s * GT + i)
+                        a3g(s * GT + i)
                     if i == 0 and s >= 1:
                         rmul(s - 1)
                 for i in two:
@@ -294,9 +323,13 @@ def tile_dispatcher_pa_kernel(tc, inv, Wk, bk, out):
         for t in pending:
             acc_e(t)
         acc_e(NT - 1)
-        bc = psp.tile([P, D], F32, name="bc", tag="ps")
-        nc.tensor.matmul(out=bc[:], lhsT=rowfirst[:], rhs=c0[:], start=True, stop=False)
-        nc.tensor.matmul(out=bc[:], lhsT=rowlast[:], rhs=clast[:], start=False, stop=False)
+        bcs = []
+        for h in range(2):
+            bc = psp.tile([P, D // 2], F32, name="bc", tag="ps")
+            bcs.append(bc)
+            cols = slice(h * D // 2, (h + 1) * D // 2)
+            nc.tensor.matmul(out=bc[:], lhsT=rowfirst[:], rhs=c0[:, cols], start=True, stop=False)
+            nc.tensor.matmul(out=bc[:], lhsT=rowlast[:], rhs=clast[:, cols], start=False, stop=False)
         redp = const.tile([P, FCH], F32, name="redp", tag="redp")
         nc.vector.tensor_reduce(out=redp[:], in_=pos[:], axis=mybir.AxisListType.X, op=ALU.add)
         redn = const.tile([P, FCH], F32, name="redn", tag="redn")
@@ -305,11 +338,12 @@ def tile_dispatcher_pa_kernel(tc, inv, Wk, bk, out):
         nc.vector.tensor_sub(out=tot[:], in0=redp[:], in1=redn[:])
         for f in range(FCH):
             nc.tensor.matmul(
-                out=bc[:, f * P : (f + 1) * P], lhsT=tot[:, f : f + 1].to_broadcast([P, P]), rhs=ident2[:],
-                start=False, stop=(f == FCH - 1),
+                out=bcs[f // 2][:, (f % 2) * P : (f % 2 + 1) * P], lhsT=tot[:, f : f + 1].to_broadcast([P, P]),
+                rhs=ident[:], is_transpose=True, start=False, stop=(f % 2 == 1),
             )
         res = const.tile([P, D], F32, name="res", tag="res")
-        nc.vector.tensor_copy(out=res[:], in_=bc[:])
-        engs = [nc.sync, nc.scalar, nc.gpsimd, nc.sync]
+        nc.vector.tensor_scalar(out=res[:, : D // 2], in0=bcs[0][:], scalar1=2.0, scalar2=None, op0=ALU.mult)
+        nc.scalar.mul(out=res[:, D // 2 :], in_=bcs[1][:], mul=2.0)
         for r in range(D // P):
-            engs[r].dma_start(out=out[r * P : (r + 1) * P, :], in_=res[:])
+            nc.sync.dma_start(out=out[r * P : (r + 1) * P, : D // 2], in_=res[:, : D // 2])
+            nc.scalar.dma_start(out=out[r * P : (r + 1) * P, D // 2 :], in_=res[:, D // 2 :])

@@ -45,6 +45,11 @@ def tile_dispatcher_pa_kernel(tc, inv, Wk, bk, out):
         accp = ctx.enter_context(tc.psum_pool(name="accp", bufs=1))
         ctx.enter_context(tc.manual_schedule())
 
+        zeros = const.tile([P, D], F32, name="zeros", tag="zeros")
+        nc.vector.memset(zeros[:], 0.0)
+        brow = const.tile([P, D], BF16, name="brow", tag="brow")
+        nc.vector.memset(brow[:], 0.0)
+        nc.scalar.dma_start(out=brow[0:1, :], in_=bk.rearrange("(a d) -> a d", a=1))
         wraw = const.tile([P, GT, D], BF16, name="wraw", tag="wraw")
         wview = Wk.rearrange("(r p) k -> p r k", p=P)
         for h in range(2):
@@ -61,14 +66,13 @@ def tile_dispatcher_pa_kernel(tc, inv, Wk, bk, out):
 
         ident = const.tile([P, P], F32, name="ident", tag="ident")
         make_identity(nc, ident[:])
-        bkt = const.tile([P, D], BF16, name="bkt", tag="bkt")
-        nc.gpsimd.dma_start(out=bkt[:], in_=bk.partition_broadcast(P))
+        ones = const.tile([P, P], BF16, name="ones", tag="ones")
+        nc.vector.memset(ones[:], 1.0)
+        bkt = const.tile([P, D], F32, name="bkt", tag="bkt")
         one = const.tile([P, 1], F32, name="one", tag="one")
         nc.vector.memset(one[:], 1.0)
         warm = const.tile([P, 1], F32, name="warm", tag="warm")
         nc.scalar.activation(out=warm[:], in_=one[:], func=ACTF.Sqrt)
-        zeros = const.tile([P, D], F32, name="zeros", tag="zeros")
-        nc.vector.memset(zeros[:], 0.0)
 
         shiftm = const.tile([P, P], F32, name="shiftm", tag="shiftm")
         nc.gpsimd.memset(shiftm[:], 0.0)
@@ -211,7 +215,7 @@ def tile_dispatcher_pa_kernel(tc, inv, Wk, bk, out):
 
         def rmul(g):
             cols = slice(g * GT, (g + 1) * GT)
-            nc.vector.tensor_mul(out=rr[:, cols], in0=rec[:, cols], in1=ssum[:, cols])
+            nc.gpsimd.tensor_tensor(out=rr[:, cols], in0=rec[:, cols], in1=ssum[:, cols], op=ALU.mult)
 
         def a4(j, dst, func):
             g, i = divmod(j, GT)
@@ -244,7 +248,7 @@ def tile_dispatcher_pa_kernel(tc, inv, Wk, bk, out):
 
         def zero_init(dst):
             nc.tensor.matmul(
-                out=dst[:].rearrange("p f n -> p (f n)"), lhsT=ident[:], rhs=zeros[:], start=True, stop=False
+                out=dst[:].rearrange("p f n -> p (f n)"), lhsT=zeros[:, :P], rhs=zeros[:], start=True, stop=False
             )
 
         zero_init(pos)
@@ -252,6 +256,9 @@ def tile_dispatcher_pa_kernel(tc, inv, Wk, bk, out):
             transposes("w", wraw, t)
             if t % 2 == 1:
                 evac("w", t // 2, on_vector=(t == 3))
+        bps = psp.tile([P, D], F32, name="bps", tag="ps")
+        nc.tensor.matmul(out=bps[:], lhsT=ones[:], rhs=brow[:], start=True, stop=True)
+        nc.vector.tensor_copy(out=bkt[:], in_=bps[:])
         for t in range(GT):
             transposes(0, raw[0], t)
             if t % 2 == 1:
@@ -273,6 +280,7 @@ def tile_dispatcher_pa_kernel(tc, inv, Wk, bk, out):
             tg = [g for g in ([2, 3] if s == 0 else [s + 3]) if g < NG]
             if s >= 1:
                 recip(s - 1)
+                rmul(s - 1)
             if s == NG:
                 c0s = psp.tile([P, D], F32, name="c0s", tag="ps")
                 nc.tensor.matmul(out=c0s[:], lhsT=shiftm[:], rhs=c0[:], start=True, stop=True)
@@ -287,8 +295,6 @@ def tile_dispatcher_pa_kernel(tc, inv, Wk, bk, out):
                     if s < NG:
                         a1(s * GT + i)
                         a3g(s * GT + i)
-                    if i == 0 and s >= 1:
-                        rmul(s - 1)
                 for i in two:
                     if 1 <= s and s + 1 < NG:
                         mm((s + 1) * GT + i)
@@ -302,8 +308,13 @@ def tile_dispatcher_pa_kernel(tc, inv, Wk, bk, out):
                             a4(NT - 1, clast, ACTF.Abs)
                 if h == 1 and s < NG:
                     r1(s)
-                for g in tg:
-                    evac(g, h)
+                if s == 0:
+                    for g in tg:
+                        evac(g, h)
+                elif h == 1:
+                    for g in tg:
+                        evac(g, 0)
+                        evac(g, 1)
             if s == 0:
                 quant_group(1)
                 for i in range(GT):

@@ -19,7 +19,7 @@ GT = 4
 NG = NT // GT
 FCH = D // P
 MX_REPEAT = 2
-G_TILES = 3
+G_TILES = 2
 EPS = 1e-8
 XCAP = EPS / D**0.5
 
@@ -47,9 +47,6 @@ def tile_dispatcher_pa_kernel(tc, inv, Wk, bk, out):
 
         zeros = const.tile([P, D], F32, name="zeros", tag="zeros")
         nc.vector.memset(zeros[:], 0.0)
-        brow = const.tile([P, D], BF16, name="brow", tag="brow")
-        nc.vector.memset(brow[:], 0.0)
-        nc.scalar.dma_start(out=brow[0:1, :], in_=bk.rearrange("(a d) -> a d", a=1))
         wraw = const.tile([P, GT, D], BF16, name="wraw", tag="wraw")
         wview = Wk.rearrange("(r p) k -> p r k", p=P)
         for h in range(2):
@@ -66,9 +63,8 @@ def tile_dispatcher_pa_kernel(tc, inv, Wk, bk, out):
 
         ident = const.tile([P, P], F32, name="ident", tag="ident")
         make_identity(nc, ident[:])
-        ones = const.tile([P, P], BF16, name="ones", tag="ones")
-        nc.vector.memset(ones[:], 1.0)
-        bkt = const.tile([P, D], F32, name="bkt", tag="bkt")
+        bkt = const.tile([P, D], BF16, name="bkt", tag="bkt")
+        nc.gpsimd.dma_start(out=bkt[:], in_=bk.partition_broadcast(P))
         one = const.tile([P, 1], F32, name="one", tag="one")
         nc.vector.memset(one[:], 1.0)
         warm = const.tile([P, 1], F32, name="warm", tag="warm")
@@ -215,7 +211,7 @@ def tile_dispatcher_pa_kernel(tc, inv, Wk, bk, out):
 
         def rmul(g):
             cols = slice(g * GT, (g + 1) * GT)
-            nc.gpsimd.tensor_tensor(out=rr[:, cols], in0=rec[:, cols], in1=ssum[:, cols], op=ALU.mult)
+            nc.vector.tensor_mul(out=rr[:, cols], in0=rec[:, cols], in1=ssum[:, cols])
 
         def a4(j, dst, func):
             g, i = divmod(j, GT)
@@ -256,9 +252,6 @@ def tile_dispatcher_pa_kernel(tc, inv, Wk, bk, out):
             transposes("w", wraw, t)
             if t % 2 == 1:
                 evac("w", t // 2, on_vector=(t == 3))
-        bps = psp.tile([P, D], F32, name="bps", tag="ps")
-        nc.tensor.matmul(out=bps[:], lhsT=ones[:], rhs=brow[:], start=True, stop=True)
-        nc.vector.tensor_copy(out=bkt[:], in_=bps[:])
         for t in range(GT):
             transposes(0, raw[0], t)
             if t % 2 == 1:
@@ -278,9 +271,8 @@ def tile_dispatcher_pa_kernel(tc, inv, Wk, bk, out):
         pending = []
         for s in range(NG + 1):
             tg = [g for g in ([2, 3] if s == 0 else [s + 3]) if g < NG]
-            if s >= 1:
+            if 1 <= s < NG:
                 recip(s - 1)
-                rmul(s - 1)
             if s == NG:
                 c0s = psp.tile([P, D], F32, name="c0s", tag="ps")
                 nc.tensor.matmul(out=c0s[:], lhsT=shiftm[:], rhs=c0[:], start=True, stop=True)
@@ -295,6 +287,8 @@ def tile_dispatcher_pa_kernel(tc, inv, Wk, bk, out):
                     if s < NG:
                         a1(s * GT + i)
                         a3g(s * GT + i)
+                    if i == 0 and 1 <= s < NG:
+                        rmul(s - 1)
                 for i in two:
                     if 1 <= s and s + 1 < NG:
                         mm((s + 1) * GT + i)
@@ -308,13 +302,8 @@ def tile_dispatcher_pa_kernel(tc, inv, Wk, bk, out):
                             a4(NT - 1, clast, ACTF.Abs)
                 if h == 1 and s < NG:
                     r1(s)
-                if s == 0:
-                    for g in tg:
-                        evac(g, h)
-                elif h == 1:
-                    for g in tg:
-                        evac(g, 0)
-                        evac(g, 1)
+                for g in tg:
+                    evac(g, h)
             if s == 0:
                 quant_group(1)
                 for i in range(GT):
@@ -325,6 +314,9 @@ def tile_dispatcher_pa_kernel(tc, inv, Wk, bk, out):
                     if t >= 0:
                         pair(t, c[t + 1 if t % 2 == 1 else t])
                         pending.append(t)
+            if s == NG - 1:
+                recip(s)
+                rmul(s)
             if s < NG:
                 a3(s)
             if s + 2 < NG:

@@ -19,7 +19,7 @@ GT = 4
 NG = NT // GT
 FCH = D // P
 MX_REPEAT = 2
-G_TILES = 2
+G_TILES = 4
 EPS = 1e-8
 XCAP = EPS / D**0.5
 
@@ -35,9 +35,9 @@ def tile_dispatcher_pa_kernel(tc, inv, Wk, bk, out):
         rawp = ctx.enter_context(tc.tile_pool(name="rawp", bufs=NG))
         grpp = ctx.enter_context(tc.tile_pool(name="grpp", bufs=3))
         codp = ctx.enter_context(tc.tile_pool(name="codp", bufs=3))
-        op = ctx.enter_context(tc.tile_pool(name="op", bufs=2))
-        xp = ctx.enter_context(tc.tile_pool(name="xp", bufs=4))
-        cp = ctx.enter_context(tc.tile_pool(name="cp", bufs=4))
+        op = ctx.enter_context(tc.tile_pool(name="op", bufs=3))
+        xp = ctx.enter_context(tc.tile_pool(name="xp", bufs=2))
+        cp = ctx.enter_context(tc.tile_pool(name="cp", bufs=6))
         ep = ctx.enter_context(tc.tile_pool(name="ep", bufs=10))
         jp = ctx.enter_context(tc.tile_pool(name="jp", bufs=2))
         tpp = ctx.enter_context(tc.psum_pool(name="tpp", bufs=2))
@@ -183,20 +183,13 @@ def tile_dispatcher_pa_kernel(tc, inv, Wk, bk, out):
             junk = jp.tile([P, D], F32, name="junk", tag="junk")
             nc.scalar.activation(out=junk[:], in_=o[g][:, i, :], func=ACTF.Square, accum_out=n2[:, j : j + 1])
 
-        def a3g(j):
-            g, i = divmod(j, GT)
-            if i == 0:
+        def clamp(g, eng, lo, hi):
+            if g not in x:
                 xt = xp.tile([P, GT, D], F32, name="x", tag="x")
                 x[g] = xt
-            if i < G_TILES:
-                nc.gpsimd.tensor_scalar(
-                    out=x[g][:, i, :], in0=o[g][:, i, :], scalar1=XCAP, scalar2=-XCAP, op0=ALU.min, op1=ALU.max
-                )
-
-        def a3(g):
-            nc.vector.tensor_scalar(
-                out=x[g][:, G_TILES:, :].rearrange("p i d -> p (i d)"),
-                in0=o[g][:, G_TILES:, :].rearrange("p i d -> p (i d)"),
+            eng.tensor_scalar(
+                out=x[g][:, lo:hi, :].rearrange("p i d -> p (i d)"),
+                in0=o[g][:, lo:hi, :].rearrange("p i d -> p (i d)"),
                 scalar1=XCAP, scalar2=-XCAP, op0=ALU.min, op1=ALU.max,
             )
 
@@ -269,13 +262,13 @@ def tile_dispatcher_pa_kernel(tc, inv, Wk, bk, out):
         zero_init(neg)
 
         pending = []
-        for s in range(NG + 1):
+        for s in range(NG + 2):
             tg = [g for g in ([2, 3] if s == 0 else [s + 3]) if g < NG]
-            if 1 <= s < NG:
-                recip(s - 1)
             if s == NG:
                 c0s = psp.tile([P, D], F32, name="c0s", tag="ps")
                 nc.tensor.matmul(out=c0s[:], lhsT=shiftm[:], rhs=c0[:], start=True, stop=True)
+            if 1 <= s < NG:
+                clamp(s - 1, nc.gpsimd, 0, G_TILES)
             for h in range(2):
                 two = (2 * h, 2 * h + 1)
                 for g in tg:
@@ -286,41 +279,43 @@ def tile_dispatcher_pa_kernel(tc, inv, Wk, bk, out):
                 for i in two:
                     if s < NG:
                         a1(s * GT + i)
-                        a3g(s * GT + i)
-                    if i == 0 and 1 <= s < NG:
-                        rmul(s - 1)
                 for i in two:
                     if 1 <= s and s + 1 < NG:
                         mm((s + 1) * GT + i)
                 for i in two:
                     if s < NG:
                         a2(s * GT + i)
-                    if i == 0 and s >= 1:
-                        a4_even((s - 1) * GT)
-                        a4_even((s - 1) * GT + 2)
-                        if s == NG:
-                            a4(NT - 1, clast, ACTF.Abs)
-                if h == 1 and s < NG:
-                    r1(s)
-                for g in tg:
-                    evac(g, h)
+                if h == 0:
+                    for g in tg:
+                        evac(g, h)
+            if s < NG:
+                r1(s)
             if s == 0:
                 quant_group(1)
                 for i in range(GT):
                     mm(GT + i)
-            pending = []
-            if s >= 1:
-                for t in range((s - 1) * GT - 1, (s - 1) * GT + 3):
-                    if t >= 0:
-                        pair(t, c[t + 1 if t % 2 == 1 else t])
-                        pending.append(t)
-            if s == NG - 1:
-                recip(s)
-                rmul(s)
-            if s < NG:
-                a3(s)
+            if s == NG:
+                clamp(s - 1, nc.vector, 0, GT)
+            elif 1 <= s < NG and G_TILES < GT:
+                clamp(s - 1, nc.vector, G_TILES, GT)
+            if 1 <= s <= NG:
+                recip(s - 1)
+                rmul(s - 1)
+                a4_even((s - 1) * GT)
+            for g in tg:
+                evac(g, 1)
+            if 1 <= s <= NG:
+                a4_even((s - 1) * GT + 2)
+                if s == NG:
+                    a4(NT - 1, clast, ACTF.Abs)
             if s + 2 < NG:
                 quant_group(s + 2)
+            pending = []
+            if s >= 2:
+                for t in range((s - 2) * GT, (s - 2) * GT + GT):
+                    if t < NT - 1:
+                        pair(t, c[t + 1 if t % 2 == 1 else t])
+                        pending.append(t)
 
         pair(NT - 1, c0s)
         for t in pending:

@@ -20,6 +20,7 @@ NG = NT // GT
 FCH = D // P
 MX_REPEAT = 2
 G_TILES = 4
+HEAD_TILES = 4
 EPS = 1e-8
 XCAP = EPS / D**0.5
 
@@ -36,7 +37,7 @@ def tile_dispatcher_pa_kernel(tc, inv, Wk, bk, out):
         grpp = ctx.enter_context(tc.tile_pool(name="grpp", bufs=3))
         codp = ctx.enter_context(tc.tile_pool(name="codp", bufs=3))
         op = ctx.enter_context(tc.tile_pool(name="op", bufs=3))
-        xp = ctx.enter_context(tc.tile_pool(name="xp", bufs=2))
+        xp = ctx.enter_context(tc.tile_pool(name="xp", bufs=3))
         cp = ctx.enter_context(tc.tile_pool(name="cp", bufs=6))
         ep = ctx.enter_context(tc.tile_pool(name="ep", bufs=10))
         jp = ctx.enter_context(tc.tile_pool(name="jp", bufs=2))
@@ -137,27 +138,28 @@ def tile_dispatcher_pa_kernel(tc, inv, Wk, bk, out):
         def quant(key, cod, sc):
             nc.vector.quantize_mx(out=cod[:].bitcast(E5X4), scales=sc[:], in_=grouped[key][:])
 
-        def quant_group(g):
-            cod = codp.tile([P, D], U32, name="codes", tag="codes", align_bytes=64)
-            sc = codp.tile([P, D], U8, name="scl", tag="scl", align_bytes=64)
-            codes[g] = cod
-            scl[g] = sc
-            if g == 0:
-                for h in range(2):
+        def quant_group(g, halves=(None,)):
+            if g not in codes:
+                cod = codp.tile([P, D], U32, name="codes", tag="codes", align_bytes=64)
+                sc = codp.tile([P, D], U8, name="scl", tag="scl", align_bytes=64)
+                codes[g] = cod
+                scl[g] = sc
+            for h in halves:
+                if h is None:
+                    quant(g, codes[g], scl[g])
+                else:
                     cols = slice(h * D // 2, (h + 1) * D // 2)
                     nc.vector.quantize_mx(
-                        out=cod[:, cols].bitcast(E5X4), scales=sc[:, cols],
+                        out=codes[g][:, cols].bitcast(E5X4), scales=scl[g][:, cols],
                         in_=grouped[g][:, h * 2 * D : (h + 1) * 2 * D],
                     )
-            else:
-                quant(g, cod, sc)
 
         def mm(j):
             g, i = divmod(j, GT)
             pt = psp.tile([P, D], F32, name="ps", tag="ps")
             ps[j] = pt
             cols = slice(i * P, (i + 1) * P)
-            for rpt in range(1 if j == 0 else MX_REPEAT):
+            for rpt in range(1 if j < HEAD_TILES else MX_REPEAT):
                 nc.tensor.matmul_mx(
                     out=pt[:],
                     lhsT=codes[g][:, cols].bitcast(E5X4),
@@ -182,6 +184,11 @@ def tile_dispatcher_pa_kernel(tc, inv, Wk, bk, out):
             g, i = divmod(j, GT)
             junk = jp.tile([P, D], F32, name="junk", tag="junk")
             nc.scalar.activation(out=junk[:], in_=o[g][:, i, :], func=ACTF.Square, accum_out=n2[:, j : j + 1])
+
+        def hold_clamp(g):
+            xt = xp.tile([P, GT, D], F32, name="x", tag="x")
+            x[g] = xt
+            nc.vector.memset(xt[:, 0, 0:1], 0.0)
 
         def clamp(g, eng, lo, hi):
             if g not in x:
@@ -240,60 +247,71 @@ def tile_dispatcher_pa_kernel(tc, inv, Wk, bk, out):
                 out=dst[:].rearrange("p f n -> p (f n)"), lhsT=zeros[:, :P], rhs=zeros[:], start=True, stop=False
             )
 
+        def tr(g, h):
+            for i in (2 * h, 2 * h + 1):
+                transposes(g, wraw if g == "w" else raw[g], i)
+
         zero_init(pos)
-        for t in range(GT):
-            transposes("w", wraw, t)
-            if t % 2 == 1:
-                evac("w", t // 2, on_vector=(t == 3))
-        for t in range(GT):
-            transposes(0, raw[0], t)
-            if t % 2 == 1:
-                evac(0, t // 2)
-        quant("w", wcodes, wscl)
-        quant_group(0)
-        for t in range(2):
-            transposes(1, raw[1], t)
-        evac(1, 0)
-        for j in range(GT):
-            mm(j)
-        for t in range(2, GT):
-            transposes(1, raw[1], t)
-        evac(1, 1)
         zero_init(neg)
+        tr("w", 0)
+        evac("w", 0)
+        tr("w", 1)
+        evac("w", 1, on_vector=True)
+        tr(0, 0)
+        evac(0, 0)
+        tr(0, 1)
+        evac(0, 1)
+        quant("w", wcodes, wscl)
+        quant_group(0, (0,))
+        mm(0)
+        mm(1)
+        tr(1, 0)
+        evac(1, 0)
+        quant_group(0, (1,))
+        mm(2)
+        mm(3)
+        tr(1, 1)
+        evac(1, 1)
 
         pending = []
         for s in range(NG + 2):
-            tg = [g for g in ([2, 3] if s == 0 else [s + 3]) if g < NG]
+            fe = s + (2 if s == 0 else 3)
             if s == NG:
                 c0s = psp.tile([P, D], F32, name="c0s", tag="ps")
                 nc.tensor.matmul(out=c0s[:], lhsT=shiftm[:], rhs=c0[:], start=True, stop=True)
             if 1 <= s < NG:
                 clamp(s - 1, nc.gpsimd, 0, G_TILES)
+            if s == 0:
+                tr(2, 0)
+                evac(2, 0)
+                tr(2, 1)
+                evac(2, 1)
             for h in range(2):
                 two = (2 * h, 2 * h + 1)
-                for g in tg:
-                    for i in two:
-                        transposes(g, raw[g], i)
+                if 1 <= s and fe < NG:
+                    tr(fe, h)
                 for t in pending[2 * h : 2 * h + 2]:
                     acc_e(t)
                 for i in two:
                     if s < NG:
                         a1(s * GT + i)
+                if s == 0 and h == 0:
+                    quant_group(1)
                 for i in two:
-                    if 1 <= s and s + 1 < NG:
+                    if s + 1 < NG:
                         mm((s + 1) * GT + i)
                 for i in two:
                     if s < NG:
                         a2(s * GT + i)
-                if h == 0:
-                    for g in tg:
-                        evac(g, h)
+                if h == 0 and 1 <= s and fe < NG:
+                    evac(fe, h)
             if s < NG:
                 r1(s)
             if s == 0:
-                quant_group(1)
-                for i in range(GT):
-                    mm(GT + i)
+                tr(3, 0)
+                evac(3, 0)
+                tr(3, 1)
+                evac(3, 1)
             if s == NG:
                 clamp(s - 1, nc.vector, 0, GT)
             elif 1 <= s < NG and G_TILES < GT:
@@ -302,8 +320,8 @@ def tile_dispatcher_pa_kernel(tc, inv, Wk, bk, out):
                 recip(s - 1)
                 rmul(s - 1)
                 a4_even((s - 1) * GT)
-            for g in tg:
-                evac(g, 1)
+            if 1 <= s and fe < NG:
+                evac(fe, 1)
             if 1 <= s <= NG:
                 a4_even((s - 1) * GT + 2)
                 if s == NG:
@@ -312,10 +330,13 @@ def tile_dispatcher_pa_kernel(tc, inv, Wk, bk, out):
                 quant_group(s + 2)
             pending = []
             if s >= 2:
-                for t in range((s - 2) * GT, (s - 2) * GT + GT):
-                    if t < NT - 1:
+                g = s - 2
+                for t in (g * GT, g * GT + 1, g * GT + 2, g * GT - 1):
+                    if t >= 0:
                         pair(t, c[t + 1 if t % 2 == 1 else t])
                         pending.append(t)
+            if s < 3:
+                hold_clamp(s)
 
         pair(NT - 1, c0s)
         for t in pending:

@@ -56,9 +56,11 @@ def tile_dispatcher_pa_kernel(tc, inv, Wk, bk, out):
         for g in range(NG):
             rt = rawp.tile([P, GT, D], BF16, name="raw", tag="raw")
             raw[g] = rt
-            if g == 0:
+            if g <= 1:
                 for h in range(2):
-                    nc.sync.dma_start(out=rt[:, 2 * h : 2 * h + 2, :], in_=flat[:, 2 * h : 2 * h + 2, :])
+                    nc.sync.dma_start(
+                        out=rt[:, 2 * h : 2 * h + 2, :], in_=flat[:, g * GT + 2 * h : g * GT + 2 * h + 2, :]
+                    )
             else:
                 nc.sync.dma_start(out=rt[:], in_=flat[:, g * GT : (g + 1) * GT, :])
 
@@ -263,22 +265,29 @@ def tile_dispatcher_pa_kernel(tc, inv, Wk, bk, out):
         evac(0, 1)
         quant("w", wcodes, wscl)
         quant_group(0, (0,))
-        mm(0)
-        mm(1)
         tr(1, 0)
         evac(1, 0)
+        mm(0)
+        mm(1)
         quant_group(0, (1,))
-        mm(2)
-        mm(3)
         tr(1, 1)
         evac(1, 1)
+        mm(2)
+        mm(3)
 
         pending = []
+        bcs = []
         for s in range(NG + 2):
             fe = s + (2 if s == 0 else 3)
             if s == NG:
                 c0s = psp.tile([P, D], F32, name="c0s", tag="ps")
                 nc.tensor.matmul(out=c0s[:], lhsT=shiftm[:], rhs=c0[:], start=True, stop=True)
+                for h in range(2):
+                    bc = psp.tile([P, D // 2], F32, name="bc", tag="ps")
+                    bcs.append(bc)
+                    nc.tensor.matmul(
+                        out=bc[:], lhsT=rowfirst[:], rhs=c0[:, h * D // 2 : (h + 1) * D // 2], start=True, stop=False
+                    )
             if 1 <= s < NG:
                 clamp(s - 1, nc.gpsimd, 0, G_TILES)
             if s == 0:
@@ -295,8 +304,8 @@ def tile_dispatcher_pa_kernel(tc, inv, Wk, bk, out):
                 for i in two:
                     if s < NG:
                         a1(s * GT + i)
-                if s == 0 and h == 0:
-                    quant_group(1)
+                if s == 0:
+                    quant_group(1, (h,))
                 for i in two:
                     if s + 1 < NG:
                         mm((s + 1) * GT + i)
@@ -319,48 +328,56 @@ def tile_dispatcher_pa_kernel(tc, inv, Wk, bk, out):
             if 1 <= s <= NG:
                 recip(s - 1)
                 rmul(s - 1)
+                if s == NG:
+                    a4(NT - 1, clast, ACTF.Abs)
+                    for h in range(2):
+                        nc.tensor.matmul(
+                            out=bcs[h][:], lhsT=rowlast[:], rhs=clast[:, h * D // 2 : (h + 1) * D // 2],
+                            start=False, stop=False,
+                        )
                 a4_even((s - 1) * GT)
             if 1 <= s and fe < NG:
                 evac(fe, 1)
             if 1 <= s <= NG:
                 a4_even((s - 1) * GT + 2)
-                if s == NG:
-                    a4(NT - 1, clast, ACTF.Abs)
             if s + 2 < NG:
                 quant_group(s + 2)
             pending = []
             if s >= 2:
                 g = s - 2
-                for t in (g * GT, g * GT + 1, g * GT + 2, g * GT - 1):
+                order = (g * GT, g * GT + 1, g * GT + 2, g * GT - 1)
+                if s == NG + 1:
+                    order = (NT - 5, NT - 3, NT - 1, NT - 4, NT - 2)
+                for t in order:
                     if t >= 0:
-                        pair(t, c[t + 1 if t % 2 == 1 else t])
+                        pair(t, c0s if t == NT - 1 else c[t + 1 if t % 2 == 1 else t])
                         pending.append(t)
             if s < 3:
                 hold_clamp(s)
 
-        pair(NT - 1, c0s)
+        def spread(col, f, last):
+            nc.tensor.matmul(
+                out=bcs[f // 2][:, (f % 2) * P : (f % 2 + 1) * P], lhsT=col.to_broadcast([P, P]),
+                rhs=ident[:], is_transpose=True, start=False, stop=last,
+            )
+
         for t in pending:
             acc_e(t)
-        acc_e(NT - 1)
-        bcs = []
-        for h in range(2):
-            bc = psp.tile([P, D // 2], F32, name="bc", tag="ps")
-            bcs.append(bc)
-            cols = slice(h * D // 2, (h + 1) * D // 2)
-            nc.tensor.matmul(out=bc[:], lhsT=rowfirst[:], rhs=c0[:, cols], start=True, stop=False)
-            nc.tensor.matmul(out=bc[:], lhsT=rowlast[:], rhs=clast[:, cols], start=False, stop=False)
-        redp = const.tile([P, FCH], F32, name="redp", tag="redp")
-        nc.vector.tensor_reduce(out=redp[:], in_=pos[:], axis=mybir.AxisListType.X, op=ALU.add)
         redn = const.tile([P, FCH], F32, name="redn", tag="redn")
-        nc.vector.tensor_reduce(out=redn[:], in_=neg[:], axis=mybir.AxisListType.X, op=ALU.add)
-        tot = const.tile([P, FCH], F32, name="tot", tag="tot")
-        nc.vector.tensor_sub(out=tot[:], in0=redp[:], in1=redn[:])
-        for f in range(FCH):
-            nc.tensor.matmul(
-                out=bcs[f // 2][:, (f % 2) * P : (f % 2 + 1) * P], lhsT=tot[:, f : f + 1].to_broadcast([P, P]),
-                rhs=ident[:], is_transpose=True, start=False, stop=(f % 2 == 1),
+        for f in reversed(range(FCH)):
+            junk = jp.tile([P, D], F32, name="junk", tag="junk")
+            nc.scalar.activation(
+                out=junk[:, :P], in_=neg[:, f, :], func=ACTF.Copy, scale=-1.0, accum_out=redn[:, f : f + 1]
             )
+            spread(redn[:, f : f + 1], f, False)
+        redp = const.tile([P, FCH], F32, name="redp", tag="redp")
         res = const.tile([P, D], F32, name="res", tag="res")
+        for h in (1, 0):
+            nc.vector.tensor_reduce(
+                out=redp[:, 2 * h : 2 * h + 2], in_=pos[:, 2 * h : 2 * h + 2, :], axis=mybir.AxisListType.X, op=ALU.add
+            )
+            for f in (2 * h, 2 * h + 1):
+                spread(redp[:, f : f + 1], f, f % 2 == 1)
         nc.vector.tensor_scalar(out=res[:, : D // 2], in0=bcs[0][:], scalar1=2.0, scalar2=None, op0=ALU.mult)
         nc.scalar.mul(out=res[:, D // 2 :], in_=bcs[1][:], mul=2.0)
         for r in range(D // P):

@@ -19,7 +19,8 @@ GT = 4
 NG = NT // GT
 FCH = D // P
 MX_REPEAT = 2
-G_TILES = 4
+G_COLS = 1856
+EARLY = 4
 HEAD_TILES = 4
 EPS = 1e-8
 XCAP = EPS / D**0.5
@@ -197,8 +198,8 @@ def tile_dispatcher_pa_kernel(tc, inv, Wk, bk, out):
                 xt = xp.tile([P, GT, D], F32, name="x", tag="x")
                 x[g] = xt
             eng.tensor_scalar(
-                out=x[g][:, lo:hi, :].rearrange("p i d -> p (i d)"),
-                in0=o[g][:, lo:hi, :].rearrange("p i d -> p (i d)"),
+                out=x[g][:].rearrange("p i d -> p (i d)")[:, lo:hi],
+                in0=o[g][:].rearrange("p i d -> p (i d)")[:, lo:hi],
                 scalar1=XCAP, scalar2=-XCAP, op0=ALU.min, op1=ALU.max,
             )
 
@@ -289,7 +290,9 @@ def tile_dispatcher_pa_kernel(tc, inv, Wk, bk, out):
                         out=bc[:], lhsT=rowfirst[:], rhs=c0[:, h * D // 2 : (h + 1) * D // 2], start=True, stop=False
                     )
             if 1 <= s < NG:
-                clamp(s - 1, nc.gpsimd, 0, G_TILES)
+                clamp(s - 1, nc.gpsimd, 0, G_COLS)
+            if EARLY <= s < NG:
+                recip(s - 1)
             if s == 0:
                 tr(2, 0)
                 evac(2, 0)
@@ -322,11 +325,12 @@ def tile_dispatcher_pa_kernel(tc, inv, Wk, bk, out):
                 tr(3, 1)
                 evac(3, 1)
             if s == NG:
-                clamp(s - 1, nc.vector, 0, GT)
-            elif 1 <= s < NG and G_TILES < GT:
-                clamp(s - 1, nc.vector, G_TILES, GT)
+                clamp(s - 1, nc.vector, 0, GT * D)
+            elif 1 <= s < NG and G_COLS < GT * D:
+                clamp(s - 1, nc.vector, G_COLS, GT * D)
             if 1 <= s <= NG:
-                recip(s - 1)
+                if s < EARLY or s == NG:
+                    recip(s - 1)
                 rmul(s - 1)
                 if s == NG:
                     a4(NT - 1, clast, ACTF.Abs)

@@ -49,6 +49,11 @@ def tile_dispatcher_pa_kernel(tc, inv, Wk, bk, out):
 
         zeros = const.tile([P, D], F32, name="zeros", tag="zeros")
         nc.vector.memset(zeros[:], 0.0)
+        bkrow = const.tile([P, D], BF16, name="bkrow", tag="bkrow")
+        nc.gpsimd.memset(bkrow[:], 0.0)
+        nc.scalar.dma_start(out=bkrow[0:1, :], in_=bk.rearrange("(o d) -> o d", o=1))
+        ones = const.tile([P, P], BF16, name="ones", tag="ones")
+        nc.vector.memset(ones[:], 1.0)
         wraw = const.tile([P, GT, D], BF16, name="wraw", tag="wraw")
         wview = Wk.rearrange("(r p) k -> p r k", p=P)
         for h in range(2):
@@ -68,7 +73,6 @@ def tile_dispatcher_pa_kernel(tc, inv, Wk, bk, out):
         ident = const.tile([P, P], F32, name="ident", tag="ident")
         make_identity(nc, ident[:])
         bkt = const.tile([P, D], BF16, name="bkt", tag="bkt")
-        nc.gpsimd.dma_start(out=bkt[:], in_=bk.partition_broadcast(P))
         one = const.tile([P, 1], F32, name="one", tag="one")
         nc.vector.memset(one[:], 1.0)
         warm = const.tile([P, 1], F32, name="warm", tag="warm")
@@ -258,6 +262,9 @@ def tile_dispatcher_pa_kernel(tc, inv, Wk, bk, out):
         zero_init(neg)
         tr("w", 0)
         evac("w", 0)
+        bps = psp.tile([P, D], F32, name="bps", tag="ps")
+        nc.tensor.matmul(out=bps[:], lhsT=ones[:], rhs=bkrow[:], start=True, stop=True)
+        nc.scalar.copy(out=bkt[:], in_=bps[:])
         tr("w", 1)
         evac("w", 1, on_vector=True)
         tr(0, 0)

@@ -18,7 +18,7 @@ NT = TOKENS // P
 GT = 4
 NG = NT // GT
 FCH = D // P
-MX_REPEAT = 2
+MX_REPEAT = 1
 G_COLS = 1856
 EARLY = 4
 HEAD_TILES = 4

@@ -20,10 +20,10 @@ NG = NT // GT
 FCH = D // P
 MX_REPEAT = 1
 G_COLS = 1856
-EARLY = 4
 HEAD_TILES = 4
 EPS = 1e-8
 XCAP = EPS / D**0.5
+TINY = 1e-34
 
 FLOPS = 2 * TOKENS * D * D
 
@@ -76,7 +76,7 @@ def tile_dispatcher_pa_kernel(tc, inv, Wk, bk, out):
         one = const.tile([P, 1], F32, name="one", tag="one")
         nc.vector.memset(one[:], 1.0)
         warm = const.tile([P, 1], F32, name="warm", tag="warm")
-        nc.scalar.activation(out=warm[:], in_=one[:], func=ACTF.Sqrt)
+        nc.scalar.activation(out=warm[:], in_=one[:], func=ACTF.Abs_reciprocal_sqrt)
 
         shiftm = const.tile([P, P], F32, name="shiftm", tag="shiftm")
         nc.gpsimd.memset(shiftm[:], 0.0)
@@ -99,8 +99,6 @@ def tile_dispatcher_pa_kernel(tc, inv, Wk, bk, out):
 
         ssum = const.tile([P, NT], F32, name="ssum", tag="ssum")
         n2 = const.tile([P, NT], F32, name="n2", tag="n2")
-        n2c = const.tile([P, NT], F32, name="n2c", tag="n2c")
-        nrm = const.tile([P, NT], F32, name="nrm", tag="nrm")
         rec = const.tile([P, NT], F32, name="rec", tag="rec")
         rr = const.tile([P, NT], F32, name="rr", tag="rr")
         c0 = const.tile([P, D], F32, name="c0", tag="c0")
@@ -209,16 +207,13 @@ def tile_dispatcher_pa_kernel(tc, inv, Wk, bk, out):
 
         def r1(g):
             cols = slice(g * GT, (g + 1) * GT)
-            nc.scalar.activation(out=n2c[:, cols], in_=n2[:, cols], func=ACTF.Relu, bias=-EPS * EPS)
-            nc.scalar.activation(out=nrm[:, cols], in_=n2c[:, cols], func=ACTF.Sqrt, scale=EPS * EPS, bias=EPS**4)
-
-        def recip(g):
-            cols = slice(g * GT, (g + 1) * GT)
-            nc.vector.reciprocal(out=rec[:, cols], in_=nrm[:, cols])
+            nc.scalar.activation(out=rec[:, cols], in_=n2[:, cols], func=ACTF.Abs_reciprocal_sqrt, bias=TINY)
 
         def rmul(g):
             cols = slice(g * GT, (g + 1) * GT)
-            nc.vector.tensor_mul(out=rr[:, cols], in0=rec[:, cols], in1=ssum[:, cols])
+            nc.vector.scalar_tensor_tensor(
+                out=rr[:, cols], in0=rec[:, cols], scalar=1.0 / EPS, in1=ssum[:, cols], op0=ALU.min, op1=ALU.mult
+            )
 
         def a4(j, dst, func):
             g, i = divmod(j, GT)
@@ -298,8 +293,6 @@ def tile_dispatcher_pa_kernel(tc, inv, Wk, bk, out):
                     )
             if 1 <= s < NG:
                 clamp(s - 1, nc.gpsimd, 0, G_COLS)
-            if EARLY <= s < NG:
-                recip(s - 1)
             if s == 0:
                 tr(2, 0)
                 evac(2, 0)
@@ -336,8 +329,6 @@ def tile_dispatcher_pa_kernel(tc, inv, Wk, bk, out):
             elif 1 <= s < NG and G_COLS < GT * D:
                 clamp(s - 1, nc.vector, G_COLS, GT * D)
             if 1 <= s <= NG:
-                if s < EARLY or s == NG:
-                    recip(s - 1)
                 rmul(s - 1)
                 if s == NG:
                     a4(NT - 1, clast, ACTF.Abs)
@@ -389,8 +380,8 @@ def tile_dispatcher_pa_kernel(tc, inv, Wk, bk, out):
             )
             for f in (2 * h, 2 * h + 1):
                 spread(redp[:, f : f + 1], f, f % 2 == 1)
-        nc.vector.tensor_scalar(out=res[:, : D // 2], in0=bcs[0][:], scalar1=2.0, scalar2=None, op0=ALU.mult)
-        nc.scalar.mul(out=res[:, D // 2 :], in_=bcs[1][:], mul=2.0)
+        nc.vector.tensor_scalar(out=res[:, : D // 2], in0=bcs[0][:], scalar1=2.0 / EPS, scalar2=None, op0=ALU.mult)
+        nc.scalar.mul(out=res[:, D // 2 :], in_=bcs[1][:], mul=2.0 / EPS)
         for r in range(D // P):
             nc.sync.dma_start(out=out[r * P : (r + 1) * P, : D // 2], in_=res[:, : D // 2])
             nc.scalar.dma_start(out=out[r * P : (r + 1) * P, D // 2 :], in_=res[:, D // 2 :])

@@ -21,6 +21,7 @@ FCH = D // P
 MX_REPEAT = 1
 G_COLS = 1856
 HEAD_TILES = 4
+H_PAIRS = (21, 33, 45, 53)
 EPS = 1e-8
 XCAP = EPS / D**0.5
 TINY = 1e-34
@@ -39,7 +40,8 @@ def tile_dispatcher_pa_kernel(tc, inv, Wk, bk, out):
         codp = ctx.enter_context(tc.tile_pool(name="codp", bufs=3))
         op = ctx.enter_context(tc.tile_pool(name="op", bufs=3))
         xp = ctx.enter_context(tc.tile_pool(name="xp", bufs=3))
-        cp = ctx.enter_context(tc.tile_pool(name="cp", bufs=6))
+        cp = ctx.enter_context(tc.tile_pool(name="cp", bufs=8))
+        hp = ctx.enter_context(tc.tile_pool(name="hp", bufs=2))
         ep = ctx.enter_context(tc.tile_pool(name="ep", bufs=10))
         jp = ctx.enter_context(tc.tile_pool(name="jp", bufs=2))
         tpp = ctx.enter_context(tc.psum_pool(name="tpp", bufs=2))
@@ -101,6 +103,7 @@ def tile_dispatcher_pa_kernel(tc, inv, Wk, bk, out):
         n2 = const.tile([P, NT], F32, name="n2", tag="n2")
         rec = const.tile([P, NT], F32, name="rec", tag="rec")
         rr = const.tile([P, NT], F32, name="rr", tag="rr")
+        nrr = const.tile([P, NT], F32, name="nrr", tag="nrr")
         c0 = const.tile([P, D], F32, name="c0", tag="c0")
         clast = const.tile([P, D], F32, name="clast", tag="clast")
         wcodes = const.tile([P, D], U32, name="wcodes", tag="wcodes", align_bytes=64)
@@ -117,6 +120,21 @@ def tile_dispatcher_pa_kernel(tc, inv, Wk, bk, out):
         x = {}
         c = {}
         e = {}
+        dif = {}
+        hrel = {}
+        bank = {}
+
+        typ = {}
+        sg = {}
+        run = 1
+        for t in range(NT):
+            if t in H_PAIRS:
+                typ[t] = -run
+                sg[t] = run
+                sg[t + 1] = -run
+            else:
+                typ[t] = run
+                run = -run
 
         def transposes(key, src, t):
             half = t // 2
@@ -217,7 +235,42 @@ def tile_dispatcher_pa_kernel(tc, inv, Wk, bk, out):
 
         def a4(j, dst, func):
             g, i = divmod(j, GT)
-            nc.scalar.activation(out=dst[:], in_=x[g][:, i, :], func=func, scale=rr[:, j : j + 1])
+            sc = rr if sg.get(j, 1) > 0 else nrr
+            nc.scalar.activation(out=dst[:], in_=x[g][:, i, :], func=func, scale=sc[:, j : j + 1])
+
+        minus = set()
+        for j in sg:
+            if sg[j] < 0:
+                minus.add(j)
+                if j % 2 == 0:
+                    for k in (j - 1, j + 1):
+                        if min(j, k) not in H_PAIRS:
+                            minus.add(k)
+
+        def negate(g):
+            if any(j // GT == g for j in minus):
+                cols = slice(g * GT, (g + 1) * GT)
+                nc.scalar.mul(out=nrr[:, cols], in_=rr[:, cols], mul=-1.0)
+
+        def hdiff(t):
+            dtile = tpp.tile([P, FCH, P], F32, name="tp", tag="tp")
+            dif[t] = dtile
+            for f in range(FCH):
+                for n, j in enumerate((t, t + 1)):
+                    nc.tensor.matmul(
+                        out=dtile[:, f, :], lhsT=c[j][:, f * P : (f + 1) * P], rhs=ident[:], is_transpose=True,
+                        start=(n == 0), stop=(n == 1),
+                    )
+
+        def hrelu(t):
+            rt = hp.tile([P, D], F32, name="hr", tag="hr")
+            hrel[t] = rt
+            nc.scalar.activation(out=rt[:], in_=dif[t][:].rearrange("p f n -> p (f n)"), func=ACTF.Relu)
+
+        def hadd(t):
+            nc.tensor.matmul(
+                out=pos[:].rearrange("p f n -> p (f n)"), lhsT=ident[:], rhs=hrel[t][:], start=False, stop=False
+            )
 
         def a4_even(j):
             if j == 0:
@@ -229,15 +282,19 @@ def tile_dispatcher_pa_kernel(tc, inv, Wk, bk, out):
 
         def pair(t, other):
             k = t if t % 2 == 1 else t + 1
+            s_a = sg.get(2 * t + 1 - k, 1)
+            is_max = typ[t] * s_a == 1
+            bank[t] = pos if is_max else neg
+            sc = rr if s_a > 0 else nrr
             et = ep.tile([P, D], F32, name="e", tag="e")
             e[t] = et
             nc.vector.scalar_tensor_tensor(
-                out=et[:], in0=x[k // GT][:, k % GT, :], scalar=rr[:, k : k + 1], in1=other[:],
-                op0=ALU.mult, op1=(ALU.max if t % 2 == 0 else ALU.min),
+                out=et[:], in0=x[k // GT][:, k % GT, :], scalar=sc[:, k : k + 1], in1=other[:],
+                op0=ALU.mult, op1=(ALU.max if is_max else ALU.min),
             )
 
         def acc_e(t):
-            dst = pos if t % 2 == 0 else neg
+            dst = bank[t]
             for f in range(FCH):
                 nc.tensor.matmul(
                     out=dst[:, f, :], lhsT=e[t][:, f * P : (f + 1) * P], rhs=ident[:], is_transpose=True,
@@ -304,6 +361,10 @@ def tile_dispatcher_pa_kernel(tc, inv, Wk, bk, out):
                     tr(fe, h)
                 for t in pending[2 * h : 2 * h + 2]:
                     acc_e(t)
+                if h == 1:
+                    for t in ((s - 3) * GT - 1, (s - 3) * GT + 1):
+                        if t in H_PAIRS:
+                            hadd(t)
                 for i in two:
                     if s < NG:
                         a1(s * GT + i)
@@ -337,11 +398,19 @@ def tile_dispatcher_pa_kernel(tc, inv, Wk, bk, out):
                             out=bcs[h][:], lhsT=rowlast[:], rhs=clast[:, h * D // 2 : (h + 1) * D // 2],
                             start=False, stop=False,
                         )
+                negate(s - 1)
                 a4_even((s - 1) * GT)
             if 1 <= s and fe < NG:
                 evac(fe, 1)
             if 1 <= s <= NG:
                 a4_even((s - 1) * GT + 2)
+                for j in ((s - 1) * GT + 1, (s - 1) * GT + 3):
+                    if j in H_PAIRS:
+                        a4_even(j)
+            for t in ((s - 2) * GT - 1, (s - 2) * GT + 1):
+                if t in H_PAIRS:
+                    hdiff(t)
+                    hrelu(t)
             if s + 2 < NG:
                 quant_group(s + 2)
             pending = []
@@ -351,7 +420,7 @@ def tile_dispatcher_pa_kernel(tc, inv, Wk, bk, out):
                 if s == NG + 1:
                     order = (NT - 5, NT - 3, NT - 1, NT - 4, NT - 2)
                 for t in order:
-                    if t >= 0:
+                    if t >= 0 and t not in H_PAIRS:
                         pair(t, c0s if t == NT - 1 else c[t + 1 if t % 2 == 1 else t])
                         pending.append(t)
             if s < 3:

@@ -19,7 +19,7 @@ GT = 4
 NG = NT // GT
 FCH = D // P
 MX_REPEAT = 1
-G_COLS = 1856
+G_COLS = 2048
 HEAD_TILES = 4
 H_PAIRS = (21, 33, 45, 53)
 EPS = 1e-8

@@ -451,6 +451,6 @@ def tile_dispatcher_pa_kernel(tc, inv, Wk, bk, out):
                 spread(redp[:, f : f + 1], f, f % 2 == 1)
         nc.vector.tensor_scalar(out=res[:, : D // 2], in0=bcs[0][:], scalar1=2.0 / EPS, scalar2=None, op0=ALU.mult)
         nc.scalar.mul(out=res[:, D // 2 :], in_=bcs[1][:], mul=2.0 / EPS)
-        for r in range(D // P):
-            nc.sync.dma_start(out=out[r * P : (r + 1) * P, : D // 2], in_=res[:, : D // 2])
-            nc.scalar.dma_start(out=out[r * P : (r + 1) * P, D // 2 :], in_=res[:, D // 2 :])
+        rows = out.rearrange("(p r) d -> p r d", r=D // P)
+        nc.sync.dma_start(out=rows[:, 0:2, :], in_=res[:].unsqueeze(1).to_broadcast([P, 2, D]))
+        nc.scalar.dma_start(out=rows[:, 2:4, :], in_=res[:].unsqueeze(1).to_broadcast([P, 2, D]))

@@ -49,10 +49,10 @@ def tile_dispatcher_pa_kernel(tc, inv, Wk, bk, out):
         accp = ctx.enter_context(tc.psum_pool(name="accp", bufs=1))
         ctx.enter_context(tc.manual_schedule())
 
+        bkrow = const.tile([P, D], BF16, name="bkrow", tag="bkrow")
+        nc.vector.memset(bkrow[:], 0.0)
         zeros = const.tile([P, D], F32, name="zeros", tag="zeros")
         nc.vector.memset(zeros[:], 0.0)
-        bkrow = const.tile([P, D], BF16, name="bkrow", tag="bkrow")
-        nc.gpsimd.memset(bkrow[:], 0.0)
         nc.scalar.dma_start(out=bkrow[0:1, :], in_=bk.rearrange("(o d) -> o d", o=1))
         ones = const.tile([P, P], BF16, name="ones", tag="ones")
         nc.vector.memset(ones[:], 1.0)

@@ -416,7 +416,7 @@ def tile_dispatcher_pa_kernel(tc, inv, Wk, bk, out):
             pending = []
             if s >= 2:
                 g = s - 2
-                order = (g * GT, g * GT + 1, g * GT + 2, g * GT - 1)
+                order = (g * GT, g * GT + 1, g * GT - 1, g * GT + 2)
                 if s == NG + 1:
                     order = (NT - 5, NT - 3, NT - 1, NT - 4, NT - 2)
                 for t in order:

@@ -64,7 +64,10 @@ def tile_dispatcher_pa_kernel(tc, inv, Wk, bk, out):
         for g in range(NG):
             rt = rawp.tile([P, GT, D], BF16, name="raw", tag="raw")
             raw[g] = rt
-            if g <= 1:
+            if g == 0:
+                for lo, hi in ((0, 1), (1, 2), (2, 4)):
+                    nc.sync.dma_start(out=rt[:, lo:hi, :], in_=flat[:, lo:hi, :])
+            elif g == 1:
                 for h in range(2):
                     nc.sync.dma_start(
                         out=rt[:, 2 * h : 2 * h + 2, :], in_=flat[:, g * GT + 2 * h : g * GT + 2 * h + 2, :]
@@ -77,6 +80,8 @@ def tile_dispatcher_pa_kernel(tc, inv, Wk, bk, out):
         bkt = const.tile([P, D], BF16, name="bkt", tag="bkt")
         one = const.tile([P, 1], F32, name="one", tag="one")
         nc.vector.memset(one[:], 1.0)
+        ones32 = const.tile([P, D], F32, name="ones32", tag="ones32")
+        nc.vector.memset(ones32[:], 1.0)
         warm = const.tile([P, 1], F32, name="warm", tag="warm")
         nc.scalar.activation(out=warm[:], in_=one[:], func=ACTF.Abs_reciprocal_sqrt)
 
@@ -92,11 +97,16 @@ def tile_dispatcher_pa_kernel(tc, inv, Wk, bk, out):
             out=rowfirst[:], in_=rowfirst[:], compare_op=ALU.is_equal, fill=0.0,
             base=0, pattern=[[0, P]], channel_multiplier=1,
         )
-        rowlast = const.tile([P, P], F32, name="rowlast", tag="rowlast")
-        nc.gpsimd.memset(rowlast[:], -0.5)
+        sel127 = const.tile([P, P], F32, name="sel127", tag="sel127")
         nc.gpsimd.affine_select(
-            out=rowlast[:], in_=rowlast[:], compare_op=ALU.is_equal, fill=0.0,
+            out=sel127[:], in_=ident[:], compare_op=ALU.is_equal, fill=0.0,
             base=-(P - 1), pattern=[[0, P]], channel_multiplier=1,
+        )
+        half127 = const.tile([P, 1], F32, name="half127", tag="half127")
+        nc.gpsimd.memset(half127[:], 0.5)
+        nc.gpsimd.affine_select(
+            out=half127[:], in_=half127[:], compare_op=ALU.is_equal, fill=1.0,
+            base=-(P - 1), pattern=[[0, 1]], channel_multiplier=1,
         )
 
         ssum = const.tile([P, NT], F32, name="ssum", tag="ssum")
@@ -105,7 +115,7 @@ def tile_dispatcher_pa_kernel(tc, inv, Wk, bk, out):
         rr = const.tile([P, NT], F32, name="rr", tag="rr")
         nrr = const.tile([P, NT], F32, name="nrr", tag="nrr")
         c0 = const.tile([P, D], F32, name="c0", tag="c0")
-        clast = const.tile([P, D], F32, name="clast", tag="clast")
+        rrlast = const.tile([P, 1], F32, name="rrlast", tag="rrlast")
         wcodes = const.tile([P, D], U32, name="wcodes", tag="wcodes", align_bytes=64)
         wscl = const.tile([P, D], U8, name="wscl", tag="wscl", align_bytes=64)
         pos = accp.tile([P, FCH, P], F32, name="pos", tag="pos")
@@ -289,7 +299,7 @@ def tile_dispatcher_pa_kernel(tc, inv, Wk, bk, out):
             et = ep.tile([P, D], F32, name="e", tag="e")
             e[t] = et
             nc.vector.scalar_tensor_tensor(
-                out=et[:], in0=x[k // GT][:, k % GT, :], scalar=sc[:, k : k + 1], in1=other[:],
+                out=et[:], in0=x[k // GT][:, k % GT, :], scalar=(rrlast[:, 0:1] if t == NT - 1 else sc[:, k : k + 1]), in1=other[:],
                 op0=ALU.mult, op1=(ALU.max if is_max else ALU.min),
             )
 
@@ -310,25 +320,59 @@ def tile_dispatcher_pa_kernel(tc, inv, Wk, bk, out):
             for i in (2 * h, 2 * h + 1):
                 transposes(g, wraw if g == "w" else raw[g], i)
 
+        def tr_one(i):
+            tp = tpp.tile([P, 2, 2, P], F32, name="tp", tag="tp")
+            tps[("one", i)] = tp
+            words = raw[0][:].bitcast(F32)
+            for u in range(2):
+                nc.tensor.transpose(tp[:, 0, u, :], words[:, i, u : D // 2 : 2], ident[:])
+
+        def evac_one(i):
+            gw = grouped[0][:].bitcast(F32)
+            dst = gw[:, (D // 2) * i : (D // 2) * (i + 1)].rearrange("p (r u) -> p r u", u=2)
+            nc.scalar.copy(out=dst, in_=tps[("one", i)][:, 0].rearrange("p u r -> p r u"))
+
+        def quant_one(i):
+            cols = slice(i * P, (i + 1) * P)
+            nc.vector.quantize_mx(
+                out=codes[0][:, cols].bitcast(E5X4), scales=scl[0][:, cols], in_=grouped[0][:, i * D : (i + 1) * D]
+            )
+
+        def quant_w(h):
+            cols = slice(h * D // 2, (h + 1) * D // 2)
+            nc.vector.quantize_mx(
+                out=wcodes[:, cols].bitcast(E5X4), scales=wscl[:, cols], in_=grouped["w"][:, h * 2 * D : (h + 1) * 2 * D]
+            )
+
         zero_init(pos)
         zero_init(neg)
+        g0t = grpp.tile([P, GT * D], BF16, name="grouped", tag="grouped", align_bytes=64)
+        grouped[0] = g0t
+        c0t = codp.tile([P, D], U32, name="codes", tag="codes", align_bytes=64)
+        s0t = codp.tile([P, D], U8, name="scl", tag="scl", align_bytes=64)
+        codes[0] = c0t
+        scl[0] = s0t
         tr("w", 0)
         evac("w", 0)
+        tr("w", 1)
+        evac("w", 1, on_vector=True)
+        quant_w(0)
+        tr_one(0)
+        evac_one(0)
         bps = psp.tile([P, D], F32, name="bps", tag="ps")
         nc.tensor.matmul(out=bps[:], lhsT=ones[:], rhs=bkrow[:], start=True, stop=True)
         nc.scalar.copy(out=bkt[:], in_=bps[:])
-        tr("w", 1)
-        evac("w", 1, on_vector=True)
-        tr(0, 0)
-        evac(0, 0)
+        tr_one(1)
+        evac_one(1)
+        quant_one(0)
+        quant_w(1)
+        quant_one(1)
         tr(0, 1)
         evac(0, 1)
-        quant("w", wcodes, wscl)
-        quant_group(0, (0,))
-        tr(1, 0)
-        evac(1, 0)
         mm(0)
         mm(1)
+        tr(1, 0)
+        evac(1, 0)
         quant_group(0, (1,))
         tr(1, 1)
         evac(1, 1)
@@ -341,7 +385,8 @@ def tile_dispatcher_pa_kernel(tc, inv, Wk, bk, out):
             fe = s + (2 if s == 0 else 3)
             if s == NG:
                 c0s = psp.tile([P, D], F32, name="c0s", tag="ps")
-                nc.tensor.matmul(out=c0s[:], lhsT=shiftm[:], rhs=c0[:], start=True, stop=True)
+                nc.tensor.matmul(out=c0s[:], lhsT=sel127[:], rhs=ones32[:], start=True, stop=False)
+                nc.tensor.matmul(out=c0s[:], lhsT=shiftm[:], rhs=c0[:], start=False, stop=True)
                 for h in range(2):
                     bc = psp.tile([P, D // 2], F32, name="bc", tag="ps")
                     bcs.append(bc)
@@ -354,10 +399,12 @@ def tile_dispatcher_pa_kernel(tc, inv, Wk, bk, out):
                 tr(2, 0)
                 evac(2, 0)
                 tr(2, 1)
-                evac(2, 1)
+            if s == 1:
+                tr(fe, 0)
+                tr(fe, 1)
             for h in range(2):
                 two = (2 * h, 2 * h + 1)
-                if 1 <= s and fe < NG:
+                if 2 <= s and fe < NG:
                     tr(fe, h)
                 for t in pending[2 * h : 2 * h + 2]:
                     acc_e(t)
@@ -378,6 +425,8 @@ def tile_dispatcher_pa_kernel(tc, inv, Wk, bk, out):
                         a2(s * GT + i)
                 if h == 0 and 1 <= s and fe < NG:
                     evac(fe, h)
+            if s == 0:
+                evac(2, 1, on_vector=True)
             if s < NG:
                 r1(s)
             if s == 0:
@@ -392,16 +441,11 @@ def tile_dispatcher_pa_kernel(tc, inv, Wk, bk, out):
             if 1 <= s <= NG:
                 rmul(s - 1)
                 if s == NG:
-                    a4(NT - 1, clast, ACTF.Abs)
-                    for h in range(2):
-                        nc.tensor.matmul(
-                            out=bcs[h][:], lhsT=rowlast[:], rhs=clast[:, h * D // 2 : (h + 1) * D // 2],
-                            start=False, stop=False,
-                        )
+                    nc.scalar.activation(out=rrlast[:], in_=rr[:, NT - 1 : NT], func=ACTF.Copy, scale=half127[:, 0:1])
                 negate(s - 1)
                 a4_even((s - 1) * GT)
             if 1 <= s and fe < NG:
-                evac(fe, 1)
+                evac(fe, 1, on_vector=(s == 1))
             if 1 <= s <= NG:
                 a4_even((s - 1) * GT + 2)
                 for j in ((s - 1) * GT + 1, (s - 1) * GT + 3):

@@ -308,7 +308,7 @@ def tile_dispatcher_pa_kernel(tc, inv, Wk, bk, out):
             for f in range(FCH):
                 nc.tensor.matmul(
                     out=dst[:, f, :], lhsT=e[t][:, f * P : (f + 1) * P], rhs=ident[:], is_transpose=True,
-                    start=False, stop=(t >= NT - 2 and f == FCH - 1),
+                    start=False, stop=(t in (NT - 1, NT - 4) and f == FCH - 1),
                 )
 
         def zero_init(dst):
@@ -476,21 +476,26 @@ def tile_dispatcher_pa_kernel(tc, inv, Wk, bk, out):
                 rhs=ident[:], is_transpose=True, start=False, stop=last,
             )
 
-        for t in pending:
+        for t in pending[:-1]:
             acc_e(t)
+        for h in (1, 0):
+            nc.tensor.matmul(
+                out=bcs[h][:], lhsT=ones32[:, :P], rhs=e[pending[-1]][:, h * D // 2 : (h + 1) * D // 2], start=False, stop=False
+            )
         redn = const.tile([P, FCH], F32, name="redn", tag="redn")
         for f in reversed(range(FCH)):
             junk = jp.tile([P, D], F32, name="junk", tag="junk")
             nc.scalar.activation(
                 out=junk[:, :P], in_=neg[:, f, :], func=ACTF.Copy, scale=-1.0, accum_out=redn[:, f : f + 1]
             )
-            spread(redn[:, f : f + 1], f, False)
         redp = const.tile([P, FCH], F32, name="redp", tag="redp")
         res = const.tile([P, D], F32, name="res", tag="res")
         for h in (1, 0):
             nc.vector.tensor_reduce(
                 out=redp[:, 2 * h : 2 * h + 2], in_=pos[:, 2 * h : 2 * h + 2, :], axis=mybir.AxisListType.X, op=ALU.add
             )
+            for f in (2 * h + 1, 2 * h):
+                spread(redn[:, f : f + 1], f, False)
             for f in (2 * h, 2 * h + 1):
                 spread(redp[:, f : f + 1], f, f % 2 == 1)
         nc.vector.tensor_scalar(out=res[:, : D // 2], in0=bcs[0][:], scalar1=2.0 / EPS, scalar2=None, op0=ALU.mult)

from contextlib import ExitStack

import concourse.mybir as mybir
from concourse.masks import make_identity

F32 = mybir.dt.float32
BF16 = mybir.dt.bfloat16
U32 = mybir.dt.uint32
U8 = mybir.dt.uint8
E5X4 = mybir.dt.float8_e5m2_x4
ALU = mybir.AluOpType
ACTF = mybir.ActivationFunctionType

P = 128
D = 512
TOKENS = 8192
NT = TOKENS // P
GT = 4
NG = NT // GT
FCH = D // P
MX_REPEAT = 1
G_COLS = 2048
HEAD_TILES = 4
H_PAIRS = (21, 33, 45, 53)
EPS = 1e-8
XCAP = EPS / D**0.5
TINY = 1e-34

FLOPS = 2 * TOKENS * D * D


def tile_dispatcher_pa_kernel(tc, inv, Wk, bk, out):
    nc = tc.nc
    flat = inv.flatten_outer_dims().rearrange("(p j) k -> p j k", j=NT)

    with ExitStack() as ctx:
        const = ctx.enter_context(tc.tile_pool(name="const", bufs=1))
        rawp = ctx.enter_context(tc.tile_pool(name="rawp", bufs=NG))
        grpp = ctx.enter_context(tc.tile_pool(name="grpp", bufs=3))
        codp = ctx.enter_context(tc.tile_pool(name="codp", bufs=3))
        op = ctx.enter_context(tc.tile_pool(name="op", bufs=3))
        xp = ctx.enter_context(tc.tile_pool(name="xp", bufs=3))
        cp = ctx.enter_context(tc.tile_pool(name="cp", bufs=8))
        hp = ctx.enter_context(tc.tile_pool(name="hp", bufs=2))
        ep = ctx.enter_context(tc.tile_pool(name="ep", bufs=10))
        jp = ctx.enter_context(tc.tile_pool(name="jp", bufs=2))
        tpp = ctx.enter_context(tc.psum_pool(name="tpp", bufs=2))
        psp = ctx.enter_context(tc.psum_pool(name="psp", bufs=4))
        accp = ctx.enter_context(tc.psum_pool(name="accp", bufs=1))
        ctx.enter_context(tc.manual_schedule())

        bkrow = const.tile([P, D], BF16, name="bkrow", tag="bkrow")
        nc.vector.memset(bkrow[:], 0.0)
        zeros = const.tile([P, D], F32, name="zeros", tag="zeros")
        nc.vector.memset(zeros[:], 0.0)
        nc.scalar.dma_start(out=bkrow[0:1, :], in_=bk.rearrange("(o d) -> o d", o=1))
        ones = const.tile([P, P], BF16, name="ones", tag="ones")
        nc.vector.memset(ones[:], 1.0)
        wraw = const.tile([P, GT, D], BF16, name="wraw", tag="wraw")
        wview = Wk.rearrange("(r p) k -> p r k", p=P)
        for h in range(2):
            nc.sync.dma_start(out=wraw[:, 2 * h : 2 * h + 2, :], in_=wview[:, 2 * h : 2 * h + 2, :])
        raw = {}
        for g in range(NG):
            rt = rawp.tile([P, GT, D], BF16, name="raw", tag="raw")
            raw[g] = rt
            if g == 0:
                for lo, hi in ((0, 1), (1, 2), (2, 4)):
                    nc.sync.dma_start(out=rt[:, lo:hi, :], in_=flat[:, lo:hi, :])
            elif g == 1:
                for h in range(2):
                    nc.sync.dma_start(
                        out=rt[:, 2 * h : 2 * h + 2, :], in_=flat[:, g * GT + 2 * h : g * GT + 2 * h + 2, :]
                    )
            else:
                nc.sync.dma_start(out=rt[:], in_=flat[:, g * GT : (g + 1) * GT, :])

        ident = const.tile([P, P], F32, name="ident", tag="ident")
        make_identity(nc, ident[:])
        bkt = const.tile([P, D], BF16, name="bkt", tag="bkt")
        one = const.tile([P, 1], F32, name="one", tag="one")
        nc.vector.memset(one[:], 1.0)
        ones32 = const.tile([P, D], F32, name="ones32", tag="ones32")
        nc.vector.memset(ones32[:], 1.0)
        warm = const.tile([P, 1], F32, name="warm", tag="warm")
        nc.scalar.activation(out=warm[:], in_=one[:], func=ACTF.Abs_reciprocal_sqrt)

        shiftm = const.tile([P, P], F32, name="shiftm", tag="shiftm")
        nc.gpsimd.memset(shiftm[:], 0.0)
        nc.gpsimd.affine_select(
            out=shiftm[:], in_=shiftm[:], compare_op=ALU.not_equal, fill=1.0,
            base=-1, pattern=[[-1, P]], channel_multiplier=1,
        )
        rowfirst = const.tile([P, P], F32, name="rowfirst", tag="rowfirst")
        nc.gpsimd.memset(rowfirst[:], -0.5)
        nc.gpsimd.affine_select(
            out=rowfirst[:], in_=rowfirst[:], compare_op=ALU.is_equal, fill=0.0,
            base=0, pattern=[[0, P]], channel_multiplier=1,
        )
        sel127 = const.tile([P, P], F32, name="sel127", tag="sel127")
        nc.gpsimd.affine_select(
            out=sel127[:], in_=ident[:], compare_op=ALU.is_equal, fill=0.0,
            base=-(P - 1), pattern=[[0, P]], channel_multiplier=1,
        )
        half127 = const.tile([P, 1], F32, name="half127", tag="half127")
        nc.gpsimd.memset(half127[:], 0.5)
        nc.gpsimd.affine_select(
            out=half127[:], in_=half127[:], compare_op=ALU.is_equal, fill=1.0,
            base=-(P - 1), pattern=[[0, 1]], channel_multiplier=1,
        )

        ssum = const.tile([P, NT], F32, name="ssum", tag="ssum")
        n2 = const.tile([P, NT], F32, name="n2", tag="n2")
        rec = const.tile([P, NT], F32, name="rec", tag="rec")
        rr = const.tile([P, NT], F32, name="rr", tag="rr")
        nrr = const.tile([P, NT], F32, name="nrr", tag="nrr")
        c0 = const.tile([P, D], F32, name="c0", tag="c0")
        rrlast = const.tile([P, 1], F32, name="rrlast", tag="rrlast")
        wcodes = const.tile([P, D], U32, name="wcodes", tag="wcodes", align_bytes=64)
        wscl = const.tile([P, D], U8, name="wscl", tag="wscl", align_bytes=64)
        pos = accp.tile([P, FCH, P], F32, name="pos", tag="pos")
        neg = accp.tile([P, FCH, P], F32, name="neg", tag="neg")

        grouped = {}
        codes = {}
        scl = {}
        tps = {}
        ps = {}
        o = {}
        x = {}
        c = {}
        e = {}
        dif = {}
        hrel = {}
        bank = {}

        typ = {}
        sg = {}
        run = 1
        for t in range(NT):
            if t in H_PAIRS:
                typ[t] = -run
                sg[t] = run
                sg[t + 1] = -run
            else:
                typ[t] = run
                run = -run

        def transposes(key, src, t):
            half = t // 2
            if t % 2 == 0:
                tp = tpp.tile([P, 2, 2, P], F32, name="tp", tag="tp")
                tps[(key, half)] = tp
            tp = tps[(key, half)]
            words = src[:].bitcast(F32)
            for u in range(2):
                nc.tensor.transpose(tp[:, t % 2, u, :], words[:, t, u : D // 2 : 2], ident[:])

        def evac(key, half, on_vector=False):
            if half == 0:
                gt = grpp.tile([P, GT * D], BF16, name="grouped", tag="grouped", align_bytes=64)
                grouped[key] = gt
            gw = grouped[key][:].bitcast(F32)
            dst = gw[:, D * half : D * (half + 1)].rearrange("p (t r u) -> p t r u", t=2, u=2)
            src = tps[(key, half)][:].rearrange("p t u r -> p t r u")
            if on_vector:
                nc.vector.tensor_copy(out=dst, in_=src)
            else:
                nc.scalar.copy(out=dst, in_=src)

        def quant(key, cod, sc):
            nc.vector.quantize_mx(out=cod[:].bitcast(E5X4), scales=sc[:], in_=grouped[key][:])

        def quant_group(g, halves=(None,)):
            if g not in codes:
                cod = codp.tile([P, D], U32, name="codes", tag="codes", align_bytes=64)
                sc = codp.tile([P, D], U8, name="scl", tag="scl", align_bytes=64)
                codes[g] = cod
                scl[g] = sc
            for h in halves:
                if h is None:
                    quant(g, codes[g], scl[g])
                else:
                    cols = slice(h * D // 2, (h + 1) * D // 2)
                    nc.vector.quantize_mx(
                        out=codes[g][:, cols].bitcast(E5X4), scales=scl[g][:, cols],
                        in_=grouped[g][:, h * 2 * D : (h + 1) * 2 * D],
                    )

        def mm(j):
            g, i = divmod(j, GT)
            pt = psp.tile([P, D], F32, name="ps", tag="ps")
            ps[j] = pt
            cols = slice(i * P, (i + 1) * P)
            for rpt in range(1 if j < HEAD_TILES else MX_REPEAT):
                nc.tensor.matmul_mx(
                    out=pt[:],
                    lhsT=codes[g][:, cols].bitcast(E5X4),
                    lhsT_scale=scl[g][:, cols],
                    rhs=wcodes[:].bitcast(E5X4),
                    rhs_scale=wscl[:],
                    start=True,
                    stop=True,
                )

        def a1(j):
            g, i = divmod(j, GT)
            if i == 0:
                ot = op.tile([P, GT, D], F32, name="o", tag="o")
                o[g] = ot
            nc.vector.scalar_tensor_tensor(
                out=o[g][:, i, :], in0=ps[j][:], scalar=1.0, in1=bkt[:],
                op0=ALU.mult, op1=ALU.add, accum_out=ssum[:, j : j + 1],
            )

        def a2(j):
            g, i = divmod(j, GT)
            junk = jp.tile([P, D], F32, name="junk", tag="junk")
            nc.scalar.activation(out=junk[:], in_=o[g][:, i, :], func=ACTF.Square, accum_out=n2[:, j : j + 1])

        def hold_clamp(g):
            xt = xp.tile([P, GT, D], F32, name="x", tag="x")
            x[g] = xt
            nc.vector.memset(xt[:, 0, 0:1], 0.0)

        def clamp(g, eng, lo, hi):
            if g not in x:
                xt = xp.tile([P, GT, D], F32, name="x", tag="x")
                x[g] = xt
            eng.tensor_scalar(
                out=x[g][:].rearrange("p i d -> p (i d)")[:, lo:hi],
                in0=o[g][:].rearrange("p i d -> p (i d)")[:, lo:hi],
                scalar1=XCAP, scalar2=-XCAP, op0=ALU.min, op1=ALU.max,
            )

        def r1(g):
            cols = slice(g * GT, (g + 1) * GT)
            nc.scalar.activation(out=rec[:, cols], in_=n2[:, cols], func=ACTF.Abs_reciprocal_sqrt, bias=TINY)

        def rmul(g):
            cols = slice(g * GT, (g + 1) * GT)
            nc.vector.scalar_tensor_tensor(
                out=rr[:, cols], in0=rec[:, cols], scalar=1.0 / EPS, in1=ssum[:, cols], op0=ALU.min, op1=ALU.mult
            )

        def a4(j, dst, func):
            g, i = divmod(j, GT)
            sc = rr if sg.get(j, 1) > 0 else nrr
            nc.scalar.activation(out=dst[:], in_=x[g][:, i, :], func=func, scale=sc[:, j : j + 1])

        minus = set()
        for j in sg:
            if sg[j] < 0:
                minus.add(j)
                if j % 2 == 0:
                    for k in (j - 1, j + 1):
                        if min(j, k) not in H_PAIRS:
                            minus.add(k)

        def negate(g):
            if any(j // GT == g for j in minus):
                cols = slice(g * GT, (g + 1) * GT)
                nc.scalar.mul(out=nrr[:, cols], in_=rr[:, cols], mul=-1.0)

        def hdiff(t):
            dtile = tpp.tile([P, FCH, P], F32, name="tp", tag="tp")
            dif[t] = dtile
            for f in range(FCH):
                for n, j in enumerate((t, t + 1)):
                    nc.tensor.matmul(
                        out=dtile[:, f, :], lhsT=c[j][:, f * P : (f + 1) * P], rhs=ident[:], is_transpose=True,
                        start=(n == 0), stop=(n == 1),
                    )

        def hrelu(t):
            rt = hp.tile([P, D], F32, name="hr", tag="hr")
            hrel[t] = rt
            nc.scalar.activation(out=rt[:], in_=dif[t][:].rearrange("p f n -> p (f n)"), func=ACTF.Relu)

        def hadd(t):
            nc.tensor.matmul(
                out=pos[:].rearrange("p f n -> p (f n)"), lhsT=ident[:], rhs=hrel[t][:], start=False, stop=False
            )

        def a4_even(j):
            if j == 0:
                c[j] = c0
            else:
                ct = cp.tile([P, D], F32, name="c", tag="c")
                c[j] = ct
            a4(j, c[j], ACTF.Copy)

        def pair(t, other):
            k = t if t % 2 == 1 else t + 1
            s_a = sg.get(2 * t + 1 - k, 1)
            is_max = typ[t] * s_a == 1
            bank[t] = pos if is_max else neg
            sc = rr if s_a > 0 else nrr
            et = ep.tile([P, D], F32, name="e", tag="e")
            e[t] = et
            nc.vector.scalar_tensor_tensor(
                out=et[:], in0=x[k // GT][:, k % GT, :], scalar=(rrlast[:, 0:1] if t == NT - 1 else sc[:, k : k + 1]), in1=other[:],
                op0=ALU.mult, op1=(ALU.max if is_max else ALU.min),
            )

        def acc_e(t):
            dst = bank[t]
            for f in range(FCH):
                nc.tensor.matmul(
                    out=dst[:, f, :], lhsT=e[t][:, f * P : (f + 1) * P], rhs=ident[:], is_transpose=True,
                    start=False, stop=(t in (NT - 1, NT - 4) and f == FCH - 1),
                )

        def zero_init(dst):
            nc.tensor.matmul(
                out=dst[:].rearrange("p f n -> p (f n)"), lhsT=zeros[:, :P], rhs=zeros[:], start=True, stop=False
            )

        def tr(g, h):
            for i in (2 * h, 2 * h + 1):
                transposes(g, wraw if g == "w" else raw[g], i)

        def tr_one(i):
            tp = tpp.tile([P, 2, 2, P], F32, name="tp", tag="tp")
            tps[("one", i)] = tp
            words = raw[0][:].bitcast(F32)
            for u in range(2):
                nc.tensor.transpose(tp[:, 0, u, :], words[:, i, u : D // 2 : 2], ident[:])

        def evac_one(i):
            gw = grouped[0][:].bitcast(F32)
            dst = gw[:, (D // 2) * i : (D // 2) * (i + 1)].rearrange("p (r u) -> p r u", u=2)
            nc.scalar.copy(out=dst, in_=tps[("one", i)][:, 0].rearrange("p u r -> p r u"))

        def quant_one(i):
            cols = slice(i * P, (i + 1) * P)
            nc.vector.quantize_mx(
                out=codes[0][:, cols].bitcast(E5X4), scales=scl[0][:, cols], in_=grouped[0][:, i * D : (i + 1) * D]
            )

        def quant_w(h):
            cols = slice(h * D // 2, (h + 1) * D // 2)
            nc.vector.quantize_mx(
                out=wcodes[:, cols].bitcast(E5X4), scales=wscl[:, cols], in_=grouped["w"][:, h * 2 * D : (h + 1) * 2 * D]
            )

        zero_init(pos)
        zero_init(neg)
        g0t = grpp.tile([P, GT * D], BF16, name="grouped", tag="grouped", align_bytes=64)
        grouped[0] = g0t
        c0t = codp.tile([P, D], U32, name="codes", tag="codes", align_bytes=64)
        s0t = codp.tile([P, D], U8, name="scl", tag="scl", align_bytes=64)
        codes[0] = c0t
        scl[0] = s0t
        tr("w", 0)
        evac("w", 0)
        tr("w", 1)
        evac("w", 1, on_vector=True)
        quant_w(0)
        tr_one(0)
        evac_one(0)
        bps = psp.tile([P, D], F32, name="bps", tag="ps")
        nc.tensor.matmul(out=bps[:], lhsT=ones[:], rhs=bkrow[:], start=True, stop=True)
        nc.scalar.copy(out=bkt[:], in_=bps[:])
        tr_one(1)
        evac_one(1)
        quant_one(0)
        quant_w(1)
        quant_one(1)
        tr(0, 1)
        evac(0, 1)
        mm(0)
        mm(1)
        tr(1, 0)
        evac(1, 0)
        quant_group(0, (1,))
        tr(1, 1)
        evac(1, 1)
        mm(2)
        mm(3)

        pending = []
        bcs = []
        for s in range(NG + 2):
            fe = s + (2 if s == 0 else 3)
            if s == NG:
                c0s = psp.tile([P, D], F32, name="c0s", tag="ps")
                nc.tensor.matmul(out=c0s[:], lhsT=sel127[:], rhs=ones32[:], start=True, stop=False)
                nc.tensor.matmul(out=c0s[:], lhsT=shiftm[:], rhs=c0[:], start=False, stop=True)
                for h in range(2):
                    bc = psp.tile([P, D // 2], F32, name="bc", tag="ps")
                    bcs.append(bc)
                    nc.tensor.matmul(
                        out=bc[:], lhsT=rowfirst[:], rhs=c0[:, h * D // 2 : (h + 1) * D // 2], start=True, stop=False
                    )
            if 1 <= s < NG:
                clamp(s - 1, nc.gpsimd, 0, G_COLS)
            if s == 0:
                tr(2, 0)
                evac(2, 0)
                tr(2, 1)
            if s == 1:
                tr(fe, 0)
                tr(fe, 1)
            for h in range(2):
                two = (2 * h, 2 * h + 1)
                if 2 <= s and fe < NG:
                    tr(fe, h)
                for t in pending[2 * h : 2 * h + 2]:
                    acc_e(t)
                if h == 1:
                    for t in ((s - 3) * GT - 1, (s - 3) * GT + 1):
                        if t in H_PAIRS:
                            hadd(t)
                for i in two:
                    if s < NG:
                        a1(s * GT + i)
                if s == 0:
                    quant_group(1, (h,))
                for i in two:
                    if s + 1 < NG:
                        mm((s + 1) * GT + i)
                for i in two:
                    if s < NG:
                        a2(s * GT + i)
                if h == 0 and 1 <= s and fe < NG:
                    evac(fe, h)
            if s == 0:
                evac(2, 1, on_vector=True)
            if s < NG:
                r1(s)
            if s == 0:
                tr(3, 0)
                evac(3, 0)
                tr(3, 1)
                evac(3, 1)
            if s == NG:
                clamp(s - 1, nc.vector, 0, GT * D)
            elif 1 <= s < NG and G_COLS < GT * D:
                clamp(s - 1, nc.vector, G_COLS, GT * D)
            if 1 <= s <= NG:
                rmul(s - 1)
                if s == NG:
                    nc.scalar.activation(out=rrlast[:], in_=rr[:, NT - 1 : NT], func=ACTF.Copy, scale=half127[:, 0:1])
                negate(s - 1)
                a4_even((s - 1) * GT)
            if 1 <= s and fe < NG:
                evac(fe, 1, on_vector=(s == 1))
            if 1 <= s <= NG:
                a4_even((s - 1) * GT + 2)
                for j in ((s - 1) * GT + 1, (s - 1) * GT + 3):
                    if j in H_PAIRS:
                        a4_even(j)
            for t in ((s - 2) * GT - 1, (s - 2) * GT + 1):
                if t in H_PAIRS:
                    hdiff(t)
                    hrelu(t)
            if s + 2 < NG:
                quant_group(s + 2)
            pending = []
            if s >= 2:
                g = s - 2
                order = (g * GT, g * GT + 1, g * GT - 1, g * GT + 2)
                if s == NG + 1:
                    order = (NT - 5, NT - 3, NT - 1, NT - 4, NT - 2)
                for t in order:
                    if t >= 0 and t not in H_PAIRS:
                        pair(t, c0s if t == NT - 1 else c[t + 1 if t % 2 == 1 else t])
                        pending.append(t)
            if s < 3:
                hold_clamp(s)

        def spread(col, f, last):
            nc.tensor.matmul(
                out=bcs[f // 2][:, (f % 2) * P : (f % 2 + 1) * P], lhsT=col.to_broadcast([P, P]),
                rhs=ident[:], is_transpose=True, start=False, stop=last,
            )

        for t in pending[:-1]:
            acc_e(t)
        for h in (1, 0):
            nc.tensor.matmul(
                out=bcs[h][:], lhsT=ones32[:, :P], rhs=e[pending[-1]][:, h * D // 2 : (h + 1) * D // 2], start=False, stop=False
            )
        redn = const.tile([P, FCH], F32, name="redn", tag="redn")
        for f in reversed(range(FCH)):
            junk = jp.tile([P, D], F32, name="junk", tag="junk")
            nc.scalar.activation(
                out=junk[:, :P], in_=neg[:, f, :], func=ACTF.Copy, scale=-1.0, accum_out=redn[:, f : f + 1]
            )
        redp = const.tile([P, FCH], F32, name="redp", tag="redp")
        res = const.tile([P, D], F32, name="res", tag="res")
        for h in (1, 0):
            nc.vector.tensor_reduce(
                out=redp[:, 2 * h : 2 * h + 2], in_=pos[:, 2 * h : 2 * h + 2, :], axis=mybir.AxisListType.X, op=ALU.add
            )
            for f in (2 * h + 1, 2 * h):
                spread(redn[:, f : f + 1], f, False)
            for f in (2 * h, 2 * h + 1):
                spread(redp[:, f : f + 1], f, f % 2 == 1)
        nc.vector.tensor_scalar(out=res[:, : D // 2], in0=bcs[0][:], scalar1=2.0 / EPS, scalar2=None, op0=ALU.mult)
        nc.scalar.mul(out=res[:, D // 2 :], in_=bcs[1][:], mul=2.0 / EPS)
        rows = out.rearrange("(p r) d -> p r d", r=D // P)
        nc.sync.dma_start(out=rows[:, 0:2, :], in_=res[:].unsqueeze(1).to_broadcast([P, 2, D]))
        nc.scalar.dma_start(out=rows[:, 2:4, :], in_=res[:].unsqueeze(1).to_broadcast([P, 2, D]))
